import numpy as np
import ml_dtypes


def mxq(x, axis, fmt="e4m3"):
    dtype, down = {"e4m3": (ml_dtypes.float8_e4m3fn, 7), "e5m2": (ml_dtypes.float8_e5m2, 14)}[fmt]
    v = np.moveaxis(np.asarray(x, np.float32).astype(ml_dtypes.bfloat16).astype(np.float64), axis, -1)
    blocks = v.reshape(v.shape[:-1] + (-1, 32))
    amax = np.abs(blocks).max(-1, keepdims=True)
    byte = np.maximum(np.where(amax > 0, np.frexp(amax)[1] - 1 + 127, 0) - down, 1)
    scale = np.exp2(byte - 127.0)
    codes = (blocks / scale).astype(np.float32).astype(dtype).astype(np.float64)
    return np.moveaxis((codes * scale).reshape(v.shape), -1, axis)


WIDE = False


def mx_kscale(k):
    if not WIDE:
        return np.ones(k)
    levels = np.array([10, -10, 5, -5, 0])
    if k % 512:
        return np.exp2(np.random.permutation(np.resize(levels, k // 32))).repeat(32)
    a = np.empty((k // 512, 16))
    for p in range(k // 512):
        a[p, :8] = np.random.permutation(np.resize(levels, 8))
        for g in range(8):
            far = levels[np.abs(levels - a[p, g]) >= 10]
            a[p, g + 8] = far[np.random.randint(len(far))]
    return np.exp2(a.ravel()).repeat(32)


BF16 = ml_dtypes.bfloat16


def bf(x):
    return np.asarray(x, np.float32).astype(BF16)


def f64(x):
    return np.asarray(x).astype(np.float64)


B, IN, HID, OUT, LAYERS, NG = 1024, 512, 1024, 512, 2, 4
GW = NG * HID


def sigmoid(v):
    return 1.0 / (1.0 + np.exp(-v))


def setup_inputs():
    s = mx_kscale(B)[:, None]
    u = mx_kscale(HID)
    x0 = bf(np.random.standard_normal((B, IN)))
    w0 = bf(np.random.standard_normal((GW, IN)) / np.sqrt(IN))
    hh = bf(np.random.standard_normal(GW) * 0.5)
    bi = bf(np.random.standard_normal(GW) * 0.3)
    bh = bf(np.random.standard_normal(GW) * 0.3)
    c0 = bf(np.random.standard_normal(HID))
    g = bf(np.random.standard_normal((B, HID)) * np.exp2(np.random.randint(-6, 1, (B, 1))) * 8.0 / s * u)
    gates = f64(x0) @ f64(w0).T + f64(hh) + (f64(bi) + f64(bh))
    return {
        "regime_vector": bf(f64(x0) * s),
        "W_ih0": bf(f64(w0) / np.tile(u, NG)[:, None]),
        "hh_gates": hh,
        "b_ih0": bi,
        "b_hh0": bh,
        "c_init": c0,
        "gates": np.asarray(gates, np.float32),
        "grad_out": g,
    }


def reference(regime_vector, W_ih0, hh_gates, b_ih0, b_hh0, c_init, gates, grad_out):
    zi, zf, zg, zo = np.split(f64(gates), NG, axis=-1)
    i, f, o = sigmoid(zi), sigmoid(zf), sigmoid(zo)
    g = np.tanh(zg)
    c0 = f64(c_init)
    tc = np.tanh(f * c0 + i * g)
    go = f64(grad_out)
    dc = go * o * (1.0 - tc * tc)
    d_i = dc * g * i * (1.0 - i)
    d_f = dc * c0 * f * (1.0 - f)
    d_g = dc * i * (1.0 - g * g)
    d_o = go * tc * o * (1.0 - o)
    dgates = np.concatenate([d_i, d_f, d_g, d_o], axis=-1)
    dx = mxq(dgates, 1, "e5m2") @ mxq(f64(W_ih0), 0, "e4m3")
    dw = mxq(dgates, 0, "e5m2").T @ mxq(f64(regime_vector), 0, "e4m3")
    return dx, dw

@@ -1,0 +1,273 @@
+from contextlib import ExitStack
+
+import concourse.masks as masks
+import concourse.mybir as mybir
+
+B, IN, HID, NG = 1024, 512, 1024, 4
+FLOPS = 2 * 2 * B * NG * HID * IN
+BYTES = 4 * B * NG * HID + 2 * B * HID + 2 * NG * HID * IN + 2 * B * IN + 2 * HID + 4 * B * IN + 4 * NG * HID * IN
+
+F32 = mybir.dt.float32
+BF16 = mybir.dt.bfloat16
+U32 = mybir.dt.uint32
+U8 = mybir.dt.uint8
+E4 = mybir.dt.float8_e4m3fn_x4
+E5 = mybir.dt.float8_e5m2_x4
+AF = mybir.ActivationFunctionType
+ALU = mybir.AluOpType
+
+P = 128
+J = 4
+WC = 256
+NSTEP = 8
+GI, GF, GG, GO = 0, 1, 2, 3
+DV_A = 88
+DV_B = 168
+DV_T = 336
+
+
+def tile_rdecommunicationlstm_pa_v_kernel(
+    tc, regime_vector, W_ih0, hh_gates, b_ih0, b_hh0, c_init, gates, grad_out, out_0, out_1
+):
+    nc = tc.nc
+    gates_v = gates.rearrange("(g p j) c -> g p j c", p=P, j=J)
+    go_v = grad_out.rearrange("(g p j) h -> g p j h", p=P, j=J)
+    w_v = W_ih0.rearrange("(q m j) n -> q m j n", m=64, j=J)
+    x_v = regime_vector.rearrange("(g p j) n -> g p j n", p=P, j=J)
+    out0_v = out_0.rearrange("(g p j) n -> g j p n", p=P, j=J)
+    out1_v = out_1.rearrange("(t m) n -> t m n", m=P)
+
+    with ExitStack() as ctx:
+        zp = ctx.enter_context(tc.tile_pool(name="zp", bufs=3))
+        tp = ctx.enter_context(tc.tile_pool(name="tp", bufs=1))
+        dzp = ctx.enter_context(tc.tile_pool(name="dzp", bufs=3))
+        ilp = ctx.enter_context(tc.tile_pool(name="ilp", bufs=4))
+        rawp = ctx.enter_context(tc.tile_pool(name="rawp", bufs=4))
+        keep = ctx.enter_context(tc.tile_pool(name="keep", bufs=1))
+        k1p = ctx.enter_context(tc.tile_pool(name="k1p", bufs=3))
+        qfp = ctx.enter_context(tc.tile_pool(name="qfp", bufs=3))
+        fcp = ctx.enter_context(tc.tile_pool(name="fcp", bufs=4))
+        outp = ctx.enter_context(tc.tile_pool(name="outp", bufs=5))
+        ps_acc = ctx.enter_context(tc.psum_pool(name="ps_acc", bufs=1))
+        ps_tp = ctx.enter_context(tc.psum_pool(name="ps_tp", bufs=2))
+        ps_o1 = ctx.enter_context(tc.psum_pool(name="ps_o1", bufs=2))
+
+        warm = keep.tile([P, 1], F32, name="warm", tag="warm")
+        nc.gpsimd.memset(warm[:], 0.0)
+        nc.scalar.activation(out=warm[:], in_=warm[:], func=AF.Tanh)
+        ident = keep.tile([P, P], F32, name="ident", tag="ident")
+        masks.make_identity(nc, ident[:])
+        ones = keep.tile([P, P], BF16, name="ones", tag="ones")
+        nc.vector.memset(ones[:], 1.0)
+        c0row = keep.tile([P, HID], BF16, name="c0row", tag="c0row")
+        nc.vector.memset(c0row[:], 0.0)
+        nc.sync.dma_start(out=c0row[0:1, :], in_=c_init.rearrange("(o n) -> o n", o=1))
+        c0b = keep.tile([P, HID], BF16, name="c0b", tag="c0b")
+
+        zt = {}
+        raws = {}
+        wcod = {}
+        xcod = {}
+        k0 = {}
+        acc = {}
+        later = []
+
+        def load(n):
+            g, hc = n // 4, n % 4
+            tl = {}
+            for gt in (GI, GG, GF, GO):
+                t = zp.tile([P, J, WC], F32, name="z%d" % gt, tag="z%d" % gt)
+                c0 = gt * HID + hc * WC
+                nc.sync.dma_start(out=t[:], in_=gates_v[g, :, :, c0:c0 + WC])
+                tl[gt] = t
+            t = zp.tile([P, J, WC], BF16, name="go", tag="go")
+            nc.sync.dma_start(out=t[:], in_=go_v[g, :, :, hc * WC:(hc + 1) * WC])
+            tl["go"] = t
+            zt[n] = tl
+
+        def load_w(hc, s):
+            t = rawp.tile([P, J, IN], BF16, name="raw", tag="raw")
+            for hf in (0, 1):
+                nc.sync.dma_start(out=t[64 * hf:64 * hf + 64, :, :], in_=w_v[(2 * s + hf) * 4 + hc])
+            raws[("w", hc, s)] = t
+
+        def load_x(g):
+            t = rawp.tile([P, J, IN], BF16, name="raw", tag="raw")
+            nc.sync.dma_start(out=t[:], in_=x_v[g])
+            raws[("x", g)] = t
+
+        def interleave(src, dv):
+            il = ilp.tile([P, IN, J], BF16, name="il", tag="il", align_bytes=64)
+            if dv > 0:
+                nc.vector.tensor_copy(out=il[:, 0:dv, :], in_=src[:, :, 0:dv].rearrange("p j c -> p c j"))
+            if dv < IN:
+                nc.scalar.copy(out=il[:, dv:IN, :], in_=src[:, :, dv:IN].rearrange("p j c -> p c j"))
+            return il
+
+        def quant(il, cod, sca, fmt):
+            nc.vector.quantize_mx(out=cod[:].bitcast(fmt), scales=sca[:], in_=il[:].rearrange("p c j -> p (c j)"))
+
+        def prep_in(key, store, nm, dv):
+            il = interleave(raws.pop(key), dv)
+            cod = keep.tile([P, IN], U32, name="c" + nm, tag="c" + nm, align_bytes=64)
+            sca = keep.tile([P, IN], U8, name="s" + nm, tag="s" + nm, align_bytes=64)
+            quant(il, cod, sca, E4)
+            store[key] = (cod, sca)
+
+        def s1(n):
+            tl = zt[n]
+            for gt, sc in ((GI, 0.5), (GG, 1.0), (GF, 0.5), (GO, 0.5)):
+                nc.scalar.activation(out=tl[gt][:], in_=tl[gt][:], func=AF.Tanh, scale=sc)
+
+        def stt(out, in0, scalar, in1, op0=ALU.add):
+            nc.vector.scalar_tensor_tensor(out=out, in0=in0, scalar=scalar, in1=in1, op0=op0, op1=ALU.mult)
+
+        def evac_out(dst_dram, src_psum, eng):
+            o = outp.tile([P, IN], F32, name="os", tag="os")
+            if eng == 0:
+                nc.scalar.copy(out=o[:], in_=src_psum[:])
+            else:
+                nc.vector.tensor_copy(out=o[:], in_=src_psum[:])
+            nc.sync.dma_start(out=dst_dram, in_=o[:])
+
+        def feature_road(n, s, dz):
+            g, hc = n // 4, n % 4
+            banks = []
+            for b in (0, 1):
+                bank = ps_tp.tile([P, 4 * P], F32, name="tpb", tag="tpb")
+                for jj in (0, 1):
+                    words = dz[:, 2 * b + jj, :].bitcast(F32)
+                    for u in (0, 1):
+                        k = 2 * jj + u
+                        nc.tensor.transpose(bank[:, k * P:(k + 1) * P], words[:, u:256:2], ident[:])
+                banks.append(bank)
+            cods = []
+            for b in (0, 1):
+                qf = qfp.tile([P, 8 * P], BF16, name="qf", tag="qf", align_bytes=64)
+                nc.scalar.copy(
+                    out=qf[:].bitcast(F32).rearrange("p (b r u) -> p b r u", b=2, u=2),
+                    in_=banks[b][:].rearrange("p (b u r) -> p b r u", b=2, u=2),
+                )
+                cods.append(qf)
+            wc, ws = wcod[("w", hc, s)]
+            for b in (0, 1):
+                fc = fcp.tile([P, 2 * P], U32, name="fc", tag="fc", align_bytes=64)
+                fs = fcp.tile([P, 2 * P], U8, name="fs", tag="fs", align_bytes=64)
+                nc.vector.quantize_mx(out=fc[:].bitcast(E5), scales=fs[:], in_=cods[b][:])
+                for jj in (0, 1):
+                    j = 2 * b + jj
+                    nc.tensor.matmul_mx(
+                        out=acc[j][:],
+                        lhsT=fc[:, jj * P:(jj + 1) * P].bitcast(E5),
+                        lhsT_scale=fs[:, jj * P:(jj + 1) * P],
+                        rhs=wc[:].bitcast(E4),
+                        rhs_scale=ws[:],
+                        start=(hc == 0 and s == 1),
+                        stop=(hc == 3 and s == 0),
+                    )
+
+        def token_road(n, s, dz, dv, both):
+            g, hc = n // 4, n % 4
+            il = interleave(dz, dv)
+            if g == 0:
+                cod = keep.tile([P, IN], U32, name="k0c%d%d" % (hc, s), tag="k0c%d%d" % (hc, s), align_bytes=64)
+                sca = keep.tile([P, IN], U8, name="k0s%d%d" % (hc, s), tag="k0s%d%d" % (hc, s), align_bytes=64)
+                quant(il, cod, sca, E5)
+                k0[(hc, s)] = (cod, sca)
+                return
+            cod = k1p.tile([P, IN], U32, name="k1c", tag="k1c", align_bytes=64)
+            sca = k1p.tile([P, IN], U8, name="k1s", tag="k1s", align_bytes=64)
+            quant(il, cod, sca, E5)
+            pair = (k0[(hc, s)], (cod, sca))
+            for mt in range(4):
+                o1 = ps_o1.tile([P, IN], F32, name="o1", tag="o1")
+                for gg in (0, 1):
+                    kc, ks = pair[gg]
+                    xc, xs = xcod[("x", gg)]
+                    nc.tensor.matmul_mx(
+                        out=o1[:],
+                        lhsT=kc[:, mt * P:(mt + 1) * P].bitcast(E5),
+                        lhsT_scale=ks[:, mt * P:(mt + 1) * P],
+                        rhs=xc[:].bitcast(E4),
+                        rhs_scale=xs[:],
+                        start=(gg == 0),
+                        stop=(gg == 1),
+                    )
+                t = (2 * s + mt // 2) * 8 + hc * 2 + mt % 2
+                evac_out(out1_v[t], o1, (mt % 2) if both else 0)
+
+        load(0)
+        load(1)
+        load_w(0, 1)
+        load_w(0, 0)
+        for h in (0, 1):
+            bank = ps_tp.tile([P, 4 * P], F32, name="tpb", tag="tpb")
+            nc.tensor.matmul(bank[:], lhsT=ones[:], rhs=c0row[:, h * 512:(h + 1) * 512], start=True, stop=True)
+            nc.scalar.copy(out=c0b[:, h * 512:(h + 1) * 512], in_=bank[:])
+        s1(0)
+
+        for n in range(NSTEP):
+            g, hc = n // 4, n % 4
+            last = n == NSTEP - 1
+            dv = DV_A if g == 0 else DV_B
+            if n + 2 < NSTEP:
+                load(n + 2)
+            if n + 1 < 4:
+                load_w(n + 1, 1)
+                load_w(n + 1, 0)
+            if n < 2:
+                load_x(n)
+            tl = zt.pop(n)
+            ai, af, gg_, ao, go = tl[GI], tl[GF], tl[GG], tl[GO], tl["go"]
+            t1 = tp.tile([P, J, WC], F32, name="t1", tag="t1")
+            t2 = tp.tile([P, J, WC], F32, name="t2", tag="t2")
+            t3 = tp.tile([P, J, WC], F32, name="t3", tag="t3")
+            t4 = tp.tile([P, J, WC], F32, name="t4", tag="t4")
+            t5 = tp.tile([P, J, WC], F32, name="t5", tag="t5")
+            c0s = c0b[:, hc * WC:(hc + 1) * WC].unsqueeze(1).to_broadcast([P, J, WC])
+
+            stt(t1[:], ai[:], 1.0, gg_[:])
+            nc.scalar.activation(out=gg_[:], in_=gg_[:], func=AF.Square, scale=0.5)
+            stt(t2[:], af[:], 1.0, c0s)
+            stt(t5[:], ao[:], 1.0, go[:])
+            nc.vector.tensor_tensor(out=t3[:], in0=t1[:], in1=t2[:], op=ALU.add)
+            nc.scalar.activation(out=t3[:], in_=t3[:], func=AF.Tanh, scale=0.5)
+            stt(t1[:], ai[:], -1.0, t1[:])
+            stt(t2[:], af[:], -1.0, t2[:])
+            nc.scalar.activation(out=t4[:], in_=t3[:], func=AF.Square)
+            if n + 1 < NSTEP:
+                s1(n + 1)
+
+            for job in later:
+                job()
+            later = []
+            if g == 0:
+                prep_in(("w", hc, 1), wcod, "w%d1" % hc, dv)
+                prep_in(("w", hc, 0), wcod, "w%d0" % hc, dv)
+            if n in (1, 2):
+                prep_in(("x", n - 1), xcod, "x%d" % (n - 1), dv)
+            if hc == 0:
+                for j in range(J):
+                    acc[j] = ps_acc.tile([P, IN], F32, name="acc%d" % j, tag="acc%d" % j)
+
+            dz0 = dzp.tile([P, J, 2 * WC], BF16, name="dz0", tag="dz0")
+            dz1 = dzp.tile([P, J, 2 * WC], BF16, name="dz1", tag="dz1")
+            stt(ao[:], ao[:], -1.0, t3[:])
+            stt(t4[:], t4[:], -1.0, t5[:])
+            stt(dz1[:, :, WC:2 * WC], ao[:], -0.25, t5[:], op0=ALU.mult)
+            stt(ai[:], ai[:], 1.0, t4[:])
+            stt(dz0[:, :, 0:WC], t1[:], 0.125, t4[:], op0=ALU.mult)
+            stt(dz1[:, :, 0:WC], gg_[:], -0.25, ai[:])
+            feature_road(n, 1, dz1)
+            if last:
+                token_road(n, 1, dz1, DV_T, True)
+            stt(dz0[:, :, WC:2 * WC], t2[:], 0.125, t4[:], op0=ALU.mult)
+            feature_road(n, 0, dz0)
+            if last:
+                token_road(n, 0, dz0, DV_T, True)
+            else:
+                later.append(lambda n=n, dz1=dz1, dv=dv: token_road(n, 1, dz1, dv, False))
+                later.append(lambda n=n, dz0=dz0, dv=dv: token_road(n, 0, dz0, dv, False))
+            if hc == 3:
+                for j in range(J):
+                    evac_out(out0_v[g, j], acc[j], j % 2)

@@ -21,9 +21,17 @@ J = 4
 WC = 256
 NSTEP = 8
 GI, GF, GG, GO = 0, 1, 2, 3
-DV_A = 88
-DV_B = 168
-DV_T = 336
+GOUT = 4
+
+DV_IT = (0, 0, 0, 0, 160, 160, 224, 336)
+JOBS = {
+    0: (("w", 0, 1), ("w", 0, 0)),
+    1: (("w", 1, 1), ("w", 1, 0)),
+    2: (("w", 2, 1), ("w", 2, 0)),
+    3: (("w", 3, 1), ("w", 3, 0)),
+    4: (("x", 0, 0), ("x", 1, 0)),
+}
+DV_JOB = {0: 0, 1: 96, 2: 128, 3: 128, 4: 128}
 
 
 def tile_rdecommunicationlstm_pa_v_kernel(
@@ -39,100 +47,139 @@ def tile_rdecommunicationlstm_pa_v_kernel(
 
     with ExitStack() as ctx:
         zp = ctx.enter_context(tc.tile_pool(name="zp", bufs=3))
-        tp = ctx.enter_context(tc.tile_pool(name="tp", bufs=1))
-        dzp = ctx.enter_context(tc.tile_pool(name="dzp", bufs=3))
+        tp = ctx.enter_context(tc.tile_pool(name="tp", bufs=2))
+        dzp = ctx.enter_context(tc.tile_pool(name="dzp", bufs=2))
         ilp = ctx.enter_context(tc.tile_pool(name="ilp", bufs=4))
-        rawp = ctx.enter_context(tc.tile_pool(name="rawp", bufs=4))
+        rawp = ctx.enter_context(tc.tile_pool(name="rawp", bufs=3))
         keep = ctx.enter_context(tc.tile_pool(name="keep", bufs=1))
-        k1p = ctx.enter_context(tc.tile_pool(name="k1p", bufs=3))
-        qfp = ctx.enter_context(tc.tile_pool(name="qfp", bufs=3))
+        k1p = ctx.enter_context(tc.tile_pool(name="k1p", bufs=4))
+        qfp = ctx.enter_context(tc.tile_pool(name="qfp", bufs=4))
         fcp = ctx.enter_context(tc.tile_pool(name="fcp", bufs=4))
-        outp = ctx.enter_context(tc.tile_pool(name="outp", bufs=5))
+        outp = ctx.enter_context(tc.tile_pool(name="outp", bufs=9))
         ps_acc = ctx.enter_context(tc.psum_pool(name="ps_acc", bufs=1))
         ps_tp = ctx.enter_context(tc.psum_pool(name="ps_tp", bufs=2))
         ps_o1 = ctx.enter_context(tc.psum_pool(name="ps_o1", bufs=2))
-
-        warm = keep.tile([P, 1], F32, name="warm", tag="warm")
-        nc.gpsimd.memset(warm[:], 0.0)
-        nc.scalar.activation(out=warm[:], in_=warm[:], func=AF.Tanh)
-        ident = keep.tile([P, P], F32, name="ident", tag="ident")
-        masks.make_identity(nc, ident[:])
-        ones = keep.tile([P, P], BF16, name="ones", tag="ones")
-        nc.vector.memset(ones[:], 1.0)
-        c0row = keep.tile([P, HID], BF16, name="c0row", tag="c0row")
-        nc.vector.memset(c0row[:], 0.0)
-        nc.sync.dma_start(out=c0row[0:1, :], in_=c_init.rearrange("(o n) -> o n", o=1))
-        c0b = keep.tile([P, HID], BF16, name="c0b", tag="c0b")
+        ctx.enter_context(tc.manual_schedule())
 
         zt = {}
+        tt = {}
+        dzt = {}
         raws = {}
-        wcod = {}
-        xcod = {}
+        ils = {}
+        opnd = {}
         k0 = {}
+        k1 = {}
         acc = {}
-        later = []
+        banks = {}
+        qfs = {}
+        fcs = {}
+        o1s = {}
 
-        def load(n):
-            g, hc = n // 4, n % 4
-            tl = {}
-            for gt in (GI, GG, GF, GO):
-                t = zp.tile([P, J, WC], F32, name="z%d" % gt, tag="z%d" % gt)
-                c0 = gt * HID + hc * WC
-                nc.sync.dma_start(out=t[:], in_=gates_v[g, :, :, c0:c0 + WC])
-                tl[gt] = t
-            t = zp.tile([P, J, WC], BF16, name="go", tag="go")
-            nc.sync.dma_start(out=t[:], in_=go_v[g, :, :, hc * WC:(hc + 1) * WC])
-            tl["go"] = t
-            zt[n] = tl
+        def ok(n):
+            return 0 <= n < NSTEP
 
-        def load_w(hc, s):
-            t = rawp.tile([P, J, IN], BF16, name="raw", tag="raw")
-            for hf in (0, 1):
-                nc.sync.dma_start(out=t[64 * hf:64 * hf + 64, :, :], in_=w_v[(2 * s + hf) * 4 + hc])
-            raws[("w", hc, s)] = t
-
-        def load_x(g):
-            t = rawp.tile([P, J, IN], BF16, name="raw", tag="raw")
-            nc.sync.dma_start(out=t[:], in_=x_v[g])
-            raws[("x", g)] = t
-
-        def interleave(src, dv):
-            il = ilp.tile([P, IN, J], BF16, name="il", tag="il", align_bytes=64)
-            if dv > 0:
-                nc.vector.tensor_copy(out=il[:, 0:dv, :], in_=src[:, :, 0:dv].rearrange("p j c -> p c j"))
-            if dv < IN:
-                nc.scalar.copy(out=il[:, dv:IN, :], in_=src[:, :, dv:IN].rearrange("p j c -> p c j"))
-            return il
-
-        def quant(il, cod, sca, fmt):
-            nc.vector.quantize_mx(out=cod[:].bitcast(fmt), scales=sca[:], in_=il[:].rearrange("p c j -> p (c j)"))
-
-        def prep_in(key, store, nm, dv):
-            il = interleave(raws.pop(key), dv)
-            cod = keep.tile([P, IN], U32, name="c" + nm, tag="c" + nm, align_bytes=64)
-            sca = keep.tile([P, IN], U8, name="s" + nm, tag="s" + nm, align_bytes=64)
-            quant(il, cod, sca, E4)
-            store[key] = (cod, sca)
-
-        def s1(n):
-            tl = zt[n]
-            for gt, sc in ((GI, 0.5), (GG, 1.0), (GF, 0.5), (GO, 0.5)):
-                nc.scalar.activation(out=tl[gt][:], in_=tl[gt][:], func=AF.Tanh, scale=sc)
+        def copy_on(eng, out, in_):
+            if eng == 0:
+                nc.scalar.copy(out=out, in_=in_)
+            else:
+                nc.vector.tensor_copy(out=out, in_=in_)
 
         def stt(out, in0, scalar, in1, op0=ALU.add):
             nc.vector.scalar_tensor_tensor(out=out, in0=in0, scalar=scalar, in1=in1, op0=op0, op1=ALU.mult)
 
-        def evac_out(dst_dram, src_psum, eng):
-            o = outp.tile([P, IN], F32, name="os", tag="os")
-            if eng == 0:
-                nc.scalar.copy(out=o[:], in_=src_psum[:])
-            else:
-                nc.vector.tensor_copy(out=o[:], in_=src_psum[:])
-            nc.sync.dma_start(out=dst_dram, in_=o[:])
-
-        def feature_road(n, s, dz):
+        def ld(n, which=(GI, GG, GF, GO, GOUT)):
+            if not ok(n):
+                return
             g, hc = n // 4, n % 4
-            banks = []
+            tl = zt.get(n, {})
+            for gt in which:
+                if gt == GOUT:
+                    t = zp.tile([P, J, WC], BF16, name="go", tag="go")
+                    nc.sync.dma_start(out=t[:], in_=go_v[g, :, :, hc * WC:(hc + 1) * WC])
+                else:
+                    t = zp.tile([P, J, WC], F32, name="z%d" % gt, tag="z%d" % gt)
+                    c0 = gt * HID + hc * WC
+                    nc.sync.dma_start(out=t[:], in_=gates_v[g, :, :, c0:c0 + WC])
+                tl[gt] = t
+            zt[n] = tl
+
+        def ld_jobs(k):
+            for job in JOBS.get(k, ()):
+                t = rawp.tile([P, J, IN], BF16, name="raw", tag="raw")
+                if job[0] == "w":
+                    for hf in (0, 1):
+                        nc.sync.dma_start(out=t[64 * hf:64 * hf + 64, :, :], in_=w_v[(2 * job[2] + hf) * 4 + job[1]])
+                else:
+                    nc.sync.dma_start(out=t[:], in_=x_v[job[1]])
+                raws[job] = t
+
+        def s1(n, i):
+            if not ok(n):
+                return
+            gt = ((GI, GG, GF, GO) if n < 3 else (GF, GO, GI, GG))[i]
+            t = zt[n][gt]
+            nc.scalar.activation(out=t[:], in_=t[:], func=AF.Tanh, scale=(1.0 if gt == GG else 0.5))
+
+        def chain_a(n):
+            if not ok(n):
+                return
+            hc = n % 4
+            tl = zt[n]
+            t = {}
+            for i in range(1, 6):
+                t[i] = tp.tile([P, J, WC], F32, name="t%d" % i, tag="t%d" % i)
+            tt[n] = t
+            c0s = c0b[:, hc * WC:(hc + 1) * WC].unsqueeze(1).to_broadcast([P, J, WC])
+            stt(t[1][:], tl[GI][:], 1.0, tl[GG][:])
+            stt(t[2][:], tl[GF][:], 1.0, c0s)
+            stt(t[5][:], tl[GO][:], 1.0, tl[GOUT][:])
+            nc.vector.tensor_tensor(out=t[3][:], in0=t[1][:], in1=t[2][:], op=ALU.add)
+            stt(t[1][:], tl[GI][:], -1.0, t[1][:])
+            stt(t[2][:], tl[GF][:], -1.0, t[2][:])
+
+        def s3(n, part):
+            if not ok(n):
+                return
+            t = tt[n]
+            gg = zt[n][GG]
+            if part == 0:
+                nc.scalar.activation(out=gg[:], in_=gg[:], func=AF.Square, scale=0.5)
+            elif part == 1:
+                nc.scalar.activation(out=t[3][:], in_=t[3][:], func=AF.Tanh, scale=0.5)
+            else:
+                nc.scalar.activation(out=t[4][:], in_=t[3][:], func=AF.Square)
+
+        def chain_b(n, which=(0, 1, 2, 3, 4, 5, 6)):
+            if not ok(n):
+                return
+            tl = zt[n]
+            t = tt[n]
+            if which[0] == 0:
+                dz0 = dzp.tile([P, J, 2 * WC], BF16, name="dz0", tag="dz0")
+                dz1 = dzp.tile([P, J, 2 * WC], BF16, name="dz1", tag="dz1")
+                dzt[n] = (dz0, dz1)
+            dz0, dz1 = dzt[n]
+            for i in which:
+                if i == 0:
+                    stt(tl[GO][:], tl[GO][:], -1.0, t[3][:])
+                elif i == 1:
+                    stt(t[4][:], t[4][:], -1.0, t[5][:])
+                elif i == 2:
+                    stt(dz1[:, :, WC:2 * WC], tl[GO][:], -0.25, t[5][:], op0=ALU.mult)
+                elif i == 3:
+                    stt(tl[GI][:], tl[GI][:], 1.0, t[4][:])
+                elif i == 4:
+                    stt(dz0[:, :, 0:WC], t[1][:], 0.125, t[4][:], op0=ALU.mult)
+                elif i == 5:
+                    stt(dz1[:, :, 0:WC], tl[GG][:], -0.25, tl[GI][:])
+                else:
+                    stt(dz0[:, :, WC:2 * WC], t[2][:], 0.125, t[4][:], op0=ALU.mult)
+
+        def tr(n, s):
+            if not ok(n):
+                return
+            dz = dzt[n][s]
+            bl = []
             for b in (0, 1):
                 bank = ps_tp.tile([P, 4 * P], F32, name="tpb", tag="tpb")
                 for jj in (0, 1):
@@ -140,24 +187,50 @@ def tile_rdecommunicationlstm_pa_v_kernel(
                     for u in (0, 1):
                         k = 2 * jj + u
                         nc.tensor.transpose(bank[:, k * P:(k + 1) * P], words[:, u:256:2], ident[:])
-                banks.append(bank)
-            cods = []
+                bl.append(bank)
+            banks[(n, s)] = bl
+
+        def ef(n, s, engs=(0, 0)):
+            if not ok(n):
+                return
+            bl = banks.pop((n, s))
+            ql = []
             for b in (0, 1):
                 qf = qfp.tile([P, 8 * P], BF16, name="qf", tag="qf", align_bytes=64)
-                nc.scalar.copy(
-                    out=qf[:].bitcast(F32).rearrange("p (b r u) -> p b r u", b=2, u=2),
-                    in_=banks[b][:].rearrange("p (b u r) -> p b r u", b=2, u=2),
+                copy_on(
+                    engs[b],
+                    qf[:].bitcast(F32).rearrange("p (b r u) -> p b r u", b=2, u=2),
+                    bl[b][:].rearrange("p (b u r) -> p b r u", b=2, u=2),
                 )
-                cods.append(qf)
-            wc, ws = wcod[("w", hc, s)]
+                ql.append(qf)
+            qfs[(n, s)] = ql
+
+        def qf_(n, s):
+            if not ok(n):
+                return
+            ql = qfs.pop((n, s))
+            fl = []
             for b in (0, 1):
                 fc = fcp.tile([P, 2 * P], U32, name="fc", tag="fc", align_bytes=64)
                 fs = fcp.tile([P, 2 * P], U8, name="fs", tag="fs", align_bytes=64)
-                nc.vector.quantize_mx(out=fc[:].bitcast(E5), scales=fs[:], in_=cods[b][:])
+                nc.vector.quantize_mx(out=fc[:].bitcast(E5), scales=fs[:], in_=ql[b][:])
+                fl.append((fc, fs))
+            fcs[(n, s)] = fl
+
+        def mf(n, s):
+            if not ok(n):
+                return
+            hc = n % 4
+            if hc == 0 and s == 1:
+                for j in range(J):
+                    acc[j] = ps_acc.tile([P, IN], F32, name="acc%d" % j, tag="acc%d" % j)
+            fl = fcs.pop((n, s))
+            wc, ws = opnd[("w", hc, s)]
+            for b in (0, 1):
+                fc, fs = fl[b]
                 for jj in (0, 1):
-                    j = 2 * b + jj
                     nc.tensor.matmul_mx(
-                        out=acc[j][:],
+                        out=acc[2 * b + jj][:],
                         lhsT=fc[:, jj * P:(jj + 1) * P].bitcast(E5),
                         lhsT_scale=fs[:, jj * P:(jj + 1) * P],
                         rhs=wc[:].bitcast(E4),
@@ -166,108 +239,226 @@ def tile_rdecommunicationlstm_pa_v_kernel(
                         stop=(hc == 3 and s == 0),
                     )
 
-        def token_road(n, s, dz, dv, both):
-            g, hc = n // 4, n % 4
-            il = interleave(dz, dv)
-            if g == 0:
-                cod = keep.tile([P, IN], U32, name="k0c%d%d" % (hc, s), tag="k0c%d%d" % (hc, s), align_bytes=64)
-                sca = keep.tile([P, IN], U8, name="k0s%d%d" % (hc, s), tag="k0s%d%d" % (hc, s), align_bytes=64)
-                quant(il, cod, sca, E5)
-                k0[(hc, s)] = (cod, sca)
-                return
-            cod = k1p.tile([P, IN], U32, name="k1c", tag="k1c", align_bytes=64)
-            sca = k1p.tile([P, IN], U8, name="k1s", tag="k1s", align_bytes=64)
-            quant(il, cod, sca, E5)
-            pair = (k0[(hc, s)], (cod, sca))
-            for mt in range(4):
-                o1 = ps_o1.tile([P, IN], F32, name="o1", tag="o1")
-                for gg in (0, 1):
-                    kc, ks = pair[gg]
-                    xc, xs = xcod[("x", gg)]
-                    nc.tensor.matmul_mx(
-                        out=o1[:],
-                        lhsT=kc[:, mt * P:(mt + 1) * P].bitcast(E5),
-                        lhsT_scale=ks[:, mt * P:(mt + 1) * P],
-                        rhs=xc[:].bitcast(E4),
-                        rhs_scale=xs[:],
-                        start=(gg == 0),
-                        stop=(gg == 1),
-                    )
-                t = (2 * s + mt // 2) * 8 + hc * 2 + mt % 2
-                evac_out(out1_v[t], o1, (mt % 2) if both else 0)
+        def store(dst, src_psum, eng):
+            o = outp.tile([P, IN], F32, name="os", tag="os")
+            copy_on(eng, o[:], src_psum[:])
+            nc.sync.dma_start(out=dst, in_=o[:])
 
-        load(0)
-        load(1)
-        load_w(0, 1)
-        load_w(0, 0)
+        def e0(g, j, eng):
+            store(out0_v[g, j], acc[j], eng)
+
+        def il_a(key, src, dv):
+            il = ilp.tile([P, IN, J], BF16, name="il", tag="il", align_bytes=64)
+            ils[key] = il
+            if dv < IN:
+                nc.scalar.copy(out=il[:, dv:IN, :], in_=src[:, :, dv:IN].rearrange("p j c -> p c j"))
+
+        def il_d(key, src, dv):
+            if dv > 0:
+                nc.vector.tensor_copy(out=ils[key][:, 0:dv, :], in_=src[:, :, 0:dv].rearrange("p j c -> p c j"))
+
+        def quant(key, cod, sca, fmt):
+            il = ils.pop(key)
+            nc.vector.quantize_mx(out=cod[:].bitcast(fmt), scales=sca[:], in_=il[:].rearrange("p c j -> p (c j)"))
+
+        def ita(n, s):
+            if ok(n):
+                il_a((n, s), dzt[n][s], DV_IT[n])
+
+        def itd(n, s):
+            if ok(n):
+                il_d((n, s), dzt[n][s], DV_IT[n])
+
+        def qt(n, s):
+            if not ok(n):
+                return
+            g, hc = n // 4, n % 4
+            if g == 0:
+                nm = "%d%d" % (hc, s)
+                cod = keep.tile([P, IN], U32, name="k0c" + nm, tag="k0c" + nm, align_bytes=64)
+                sca = keep.tile([P, IN], U8, name="k0s" + nm, tag="k0s" + nm, align_bytes=64)
+                k0[(hc, s)] = (cod, sca)
+            else:
+                cod = k1p.tile([P, IN], U32, name="k1c", tag="k1c", align_bytes=64)
+                sca = k1p.tile([P, IN], U8, name="k1s", tag="k1s", align_bytes=64)
+                k1[(hc, s)] = (cod, sca)
+            quant((n, s), cod, sca, E5)
+
+        def mt(n, i):
+            if not ok(n) or n < 4:
+                return
+            hc = n % 4
+            s, m = 1 - i // 4, i % 4
+            if n == NSTEP - 1 and i % 2 == 1:
+                o1 = ps_tp.tile([P, IN], F32, name="tpb", tag="tpb")
+            else:
+                o1 = ps_o1.tile([P, IN], F32, name="o1", tag="o1")
+            for gg in (0, 1):
+                kc, ks = (k0 if gg == 0 else k1)[(hc, s)]
+                xc, xs = opnd[("x", gg, 0)]
+                nc.tensor.matmul_mx(
+                    out=o1[:],
+                    lhsT=kc[:, m * P:(m + 1) * P].bitcast(E5),
+                    lhsT_scale=ks[:, m * P:(m + 1) * P],
+                    rhs=xc[:].bitcast(E4),
+                    rhs_scale=xs[:],
+                    start=(gg == 0),
+                    stop=(gg == 1),
+                )
+            o1s[(n, i)] = o1
+
+        def eo(n, i, eng=0):
+            if not ok(n) or n < 4:
+                return
+            hc = n % 4
+            s, m = 1 - i // 4, i % 4
+            store(out1_v[(2 * s + m // 2) * 8 + hc * 2 + m % 2], o1s.pop((n, i)), eng)
+
+        def jobs_a(k):
+            for job in JOBS.get(k, ()):
+                il_a(job, raws[job], DV_JOB[k])
+
+        def jobs_d(k):
+            for job in JOBS.get(k, ()):
+                il_d(job, raws.pop(job), DV_JOB[k])
+
+        def jobs_q(k):
+            for job in JOBS.get(k, ()):
+                nm = "%s%d%d" % job
+                cod = keep.tile([P, IN], U32, name="c" + nm, tag="c" + nm, align_bytes=64)
+                sca = keep.tile([P, IN], U8, name="s" + nm, tag="s" + nm, align_bytes=64)
+                quant(job, cod, sca, E4)
+                opnd[job] = (cod, sca)
+
+        c0row = keep.tile([P, HID], BF16, name="c0row", tag="c0row")
+        nc.vector.memset(c0row[:], 0.0)
+        nc.sync.dma_start(out=c0row[0:1, :], in_=c_init.rearrange("(o n) -> o n", o=1))
+        ld(0)
+        warm = keep.tile([P, 1], F32, name="warm", tag="warm")
+        nc.gpsimd.memset(warm[:], 0.0)
+        nc.scalar.activation(out=warm[:], in_=warm[:], func=AF.Tanh)
+        ones = keep.tile([P, P], BF16, name="ones", tag="ones")
+        nc.vector.memset(ones[:], 1.0)
+        ident = keep.tile([P, P], F32, name="ident", tag="ident")
+        masks.make_identity(nc, ident[:])
+        c0b = keep.tile([P, HID], BF16, name="c0b", tag="c0b")
         for h in (0, 1):
             bank = ps_tp.tile([P, 4 * P], F32, name="tpb", tag="tpb")
             nc.tensor.matmul(bank[:], lhsT=ones[:], rhs=c0row[:, h * 512:(h + 1) * 512], start=True, stop=True)
-            nc.scalar.copy(out=c0b[:, h * 512:(h + 1) * 512], in_=bank[:])
-        s1(0)
+            nc.vector.tensor_copy(out=c0b[:, h * 512:(h + 1) * 512], in_=bank[:])
+        ld(1)
+        ld(2)
+        ld_jobs(0)
 
-        for n in range(NSTEP):
-            g, hc = n // 4, n % 4
-            last = n == NSTEP - 1
-            dv = DV_A if g == 0 else DV_B
-            if n + 2 < NSTEP:
-                load(n + 2)
-            if n + 1 < 4:
-                load_w(n + 1, 1)
-                load_w(n + 1, 0)
-            if n < 2:
-                load_x(n)
-            tl = zt.pop(n)
-            ai, af, gg_, ao, go = tl[GI], tl[GF], tl[GG], tl[GO], tl["go"]
-            t1 = tp.tile([P, J, WC], F32, name="t1", tag="t1")
-            t2 = tp.tile([P, J, WC], F32, name="t2", tag="t2")
-            t3 = tp.tile([P, J, WC], F32, name="t3", tag="t3")
-            t4 = tp.tile([P, J, WC], F32, name="t4", tag="t4")
-            t5 = tp.tile([P, J, WC], F32, name="t5", tag="t5")
-            c0s = c0b[:, hc * WC:(hc + 1) * WC].unsqueeze(1).to_broadcast([P, J, WC])
+        for k in range(-2, NSTEP - 1):
+            if k >= 0:
+                ld(k + 3, (GF, GOUT))
+            ef(k - 1, 1)
+            tr(k - 1, 0)
+            ita(k - 1, 1)
+            ita(k - 1, 0)
+            itd(k - 1, 1)
+            itd(k - 1, 0)
+            chain_a(k + 1)
+            ef(k - 1, 0)
+            s1(k + 2, 0)
+            s1(k + 2, 1)
+            qt(k - 1, 1)
+            qt(k - 1, 0)
+            mt(k - 1, 0)
+            mt(k - 1, 1)
+            chain_b(k)
+            s1(k + 2, 2)
+            eo(k - 1, 0)
+            mt(k - 1, 2)
+            s1(k + 2, 3)
+            eo(k - 1, 1)
+            mt(k - 1, 3)
+            if k == 5:
+                e0(0, 0, 0)
+                e0(0, 1, 0)
+                e0(0, 2, 0)
+                e0(0, 3, 0)
+            eo(k - 1, 2)
+            mt(k - 1, 4)
+            if k >= 0:
+                ld(k + 3, (GO,))
+            jobs_a(k)
+            s3(k + 1, 0)
+            eo(k - 1, 3)
+            mt(k - 1, 5)
+            s3(k + 1, 1)
+            eo(k - 1, 4)
+            mt(k - 1, 6)
+            s3(k + 1, 2)
+            eo(k - 1, 5)
+            mt(k - 1, 7)
+            if k >= 0:
+                ld(k + 3, (GI, GG))
+            eo(k - 1, 6)
+            eo(k - 1, 7)
+            tr(k, 1)
+            jobs_d(k)
+            qf_(k - 1, 1)
+            qf_(k - 1, 0)
+            mf(k - 1, 1)
+            mf(k - 1, 0)
+            jobs_q(k)
+            if k >= 0:
+                ld_jobs(k + 1)
 
-            stt(t1[:], ai[:], 1.0, gg_[:])
-            nc.scalar.activation(out=gg_[:], in_=gg_[:], func=AF.Square, scale=0.5)
-            stt(t2[:], af[:], 1.0, c0s)
-            stt(t5[:], ao[:], 1.0, go[:])
-            nc.vector.tensor_tensor(out=t3[:], in0=t1[:], in1=t2[:], op=ALU.add)
-            nc.scalar.activation(out=t3[:], in_=t3[:], func=AF.Tanh, scale=0.5)
-            stt(t1[:], ai[:], -1.0, t1[:])
-            stt(t2[:], af[:], -1.0, t2[:])
-            nc.scalar.activation(out=t4[:], in_=t3[:], func=AF.Square)
-            if n + 1 < NSTEP:
-                s1(n + 1)
-
-            for job in later:
-                job()
-            later = []
-            if g == 0:
-                prep_in(("w", hc, 1), wcod, "w%d1" % hc, dv)
-                prep_in(("w", hc, 0), wcod, "w%d0" % hc, dv)
-            if n in (1, 2):
-                prep_in(("x", n - 1), xcod, "x%d" % (n - 1), dv)
-            if hc == 0:
-                for j in range(J):
-                    acc[j] = ps_acc.tile([P, IN], F32, name="acc%d" % j, tag="acc%d" % j)
-
-            dz0 = dzp.tile([P, J, 2 * WC], BF16, name="dz0", tag="dz0")
-            dz1 = dzp.tile([P, J, 2 * WC], BF16, name="dz1", tag="dz1")
-            stt(ao[:], ao[:], -1.0, t3[:])
-            stt(t4[:], t4[:], -1.0, t5[:])
-            stt(dz1[:, :, WC:2 * WC], ao[:], -0.25, t5[:], op0=ALU.mult)
-            stt(ai[:], ai[:], 1.0, t4[:])
-            stt(dz0[:, :, 0:WC], t1[:], 0.125, t4[:], op0=ALU.mult)
-            stt(dz1[:, :, 0:WC], gg_[:], -0.25, ai[:])
-            feature_road(n, 1, dz1)
-            if last:
-                token_road(n, 1, dz1, DV_T, True)
-            stt(dz0[:, :, WC:2 * WC], t2[:], 0.125, t4[:], op0=ALU.mult)
-            feature_road(n, 0, dz0)
-            if last:
-                token_road(n, 0, dz0, DV_T, True)
-            else:
-                later.append(lambda n=n, dz1=dz1, dv=dv: token_road(n, 1, dz1, dv, False))
-                later.append(lambda n=n, dz0=dz0, dv=dv: token_road(n, 0, dz0, dv, False))
-            if hc == 3:
-                for j in range(J):
-                    evac_out(out0_v[g, j], acc[j], j % 2)
+        ef(6, 1)
+        tr(6, 0)
+        ita(6, 1)
+        ita(6, 0)
+        itd(6, 1)
+        itd(6, 0)
+        chain_b(7, (0, 1, 2, 3))
+        qt(6, 1)
+        mt(6, 0)
+        mt(6, 1)
+        chain_b(7, (5,))
+        ef(6, 0)
+        tr(7, 1)
+        qf_(6, 1)
+        mf(6, 1)
+        chain_b(7, (4,))
+        qt(6, 0)
+        eo(6, 0)
+        mt(6, 2)
+        eo(6, 1)
+        mt(6, 3)
+        ef(7, 1)
+        ita(7, 1)
+        itd(7, 1)
+        chain_b(7, (6,))
+        tr(7, 0)
+        qf_(7, 1)
+        qt(7, 1)
+        mf(7, 1)
+        eo(6, 2)
+        mt(6, 4)
+        eo(6, 3)
+        mt(6, 5)
+        qf_(6, 0)
+        mf(6, 0)
+        ef(7, 0, (0, 1))
+        ita(7, 0)
+        itd(7, 0)
+        eo(6, 4)
+        mt(6, 6)
+        eo(6, 5)
+        mt(6, 7)
+        qf_(7, 0)
+        qt(7, 0)
+        mf(7, 0)
+        eo(6, 6, 0)
+        eo(6, 7, 0)
+        for i in range(4):
+            mt(7, i)
+        for j in range(J):
+            e0(1, j, 1 - j % 2)
+        for i in range(8):
+            eo(7, i, i % 2)
+            if i + 4 < 8:
+                mt(7, i + 4)

@@ -23,7 +23,7 @@ NSTEP = 8
 GI, GF, GG, GO = 0, 1, 2, 3
 GOUT = 4
 
-DV_IT = (0, 0, 0, 0, 160, 160, 224, 336)
+DV_IT = (32, 32, 32, 32, 160, 160, 224, 336)
 JOBS = {
     0: (("w", 0, 1), ("w", 0, 0)),
     1: (("w", 1, 1), ("w", 1, 0)),
@@ -87,20 +87,19 @@ def tile_rdecommunicationlstm_pa_v_kernel(
         def stt(out, in0, scalar, in1, op0=ALU.add):
             nc.vector.scalar_tensor_tensor(out=out, in0=in0, scalar=scalar, in1=in1, op0=op0, op1=ALU.mult)
 
-        def ld(n, which=(GI, GG, GF, GO, GOUT)):
+        def ld(n, which=(GI, GG, GF, GO, GOUT), j0=0, j1=J):
             if not ok(n):
                 return
             g, hc = n // 4, n % 4
             tl = zt.get(n, {})
             for gt in which:
+                if gt not in tl:
+                    tl[gt] = zp.tile([P, J, WC], BF16 if gt == GOUT else F32, name="z%d" % gt, tag="z%d" % gt)
                 if gt == GOUT:
-                    t = zp.tile([P, J, WC], BF16, name="go", tag="go")
-                    nc.sync.dma_start(out=t[:], in_=go_v[g, :, :, hc * WC:(hc + 1) * WC])
+                    nc.sync.dma_start(out=tl[gt][:, j0:j1, :], in_=go_v[g, :, j0:j1, hc * WC:(hc + 1) * WC])
                 else:
-                    t = zp.tile([P, J, WC], F32, name="z%d" % gt, tag="z%d" % gt)
                     c0 = gt * HID + hc * WC
-                    nc.sync.dma_start(out=t[:], in_=gates_v[g, :, :, c0:c0 + WC])
-                tl[gt] = t
+                    nc.sync.dma_start(out=tl[gt][:, j0:j1, :], in_=gates_v[g, :, j0:j1, c0:c0 + WC])
             zt[n] = tl
 
         def ld_jobs(k):
@@ -113,29 +112,42 @@ def tile_rdecommunicationlstm_pa_v_kernel(
                     nc.sync.dma_start(out=t[:], in_=x_v[job[1]])
                 raws[job] = t
 
-        def s1(n, i):
+        def s1(n, i, j0=0, j1=J):
             if not ok(n):
                 return
             gt = ((GI, GG, GF, GO) if n < 3 else (GF, GO, GI, GG))[i]
-            t = zt[n][gt]
-            nc.scalar.activation(out=t[:], in_=t[:], func=AF.Tanh, scale=(1.0 if gt == GG else 0.5))
+            t = zt[n][gt][:, j0:j1, :]
+            nc.scalar.activation(out=t, in_=t, func=AF.Tanh, scale=(1.0 if gt == GG else 0.5))
 
-        def chain_a(n):
+        def chain_a(n, which=(0, 1, 2, 3, 4, 5), j0=0, j1=J):
             if not ok(n):
                 return
             hc = n % 4
-            tl = zt[n]
+            if n not in tt:
+                tn = {}
+                for i in range(1, 6):
+                    tn[i] = tp.tile([P, J, WC], F32, name="t%d" % i, tag="t%d" % i)
+                tt[n] = tn
             t = {}
             for i in range(1, 6):
-                t[i] = tp.tile([P, J, WC], F32, name="t%d" % i, tag="t%d" % i)
-            tt[n] = t
-            c0s = c0b[:, hc * WC:(hc + 1) * WC].unsqueeze(1).to_broadcast([P, J, WC])
-            stt(t[1][:], tl[GI][:], 1.0, tl[GG][:])
-            stt(t[2][:], tl[GF][:], 1.0, c0s)
-            stt(t[5][:], tl[GO][:], 1.0, tl[GOUT][:])
-            nc.vector.tensor_tensor(out=t[3][:], in0=t[1][:], in1=t[2][:], op=ALU.add)
-            stt(t[1][:], tl[GI][:], -1.0, t[1][:])
-            stt(t[2][:], tl[GF][:], -1.0, t[2][:])
+                t[i] = tt[n][i][:, j0:j1, :]
+            z = {}
+            for gt in (GI, GF, GG, GO, GOUT):
+                z[gt] = zt[n][gt][:, j0:j1, :]
+            c0s = c0b[:, hc * WC:(hc + 1) * WC].unsqueeze(1).to_broadcast([P, j1 - j0, WC])
+            for i in which:
+                if i == 0:
+                    stt(t[1], z[GI], 1.0, z[GG])
+                elif i == 1:
+                    stt(t[2], z[GF], 1.0, c0s)
+                elif i == 2:
+                    stt(t[5], z[GO], 1.0, z[GOUT])
+                elif i == 3:
+                    nc.vector.tensor_tensor(out=t[3], in0=t[1], in1=t[2], op=ALU.add)
+                elif i == 4:
+                    stt(t[1], z[GI], -1.0, t[1])
+                else:
+                    stt(t[2], z[GF], -1.0, t[2])
 
         def s3(n, part):
             if not ok(n):
@@ -251,11 +263,17 @@ def tile_rdecommunicationlstm_pa_v_kernel(
             il = ilp.tile([P, IN, J], BF16, name="il", tag="il", align_bytes=64)
             ils[key] = il
             if dv < IN:
-                nc.scalar.copy(out=il[:, dv:IN, :], in_=src[:, :, dv:IN].rearrange("p j c -> p c j"))
+                nc.scalar.copy(
+                    out=il[:, dv:IN, :].rearrange("p (c i) j -> p c j i", i=4),
+                    in_=src[:, :, dv:IN].rearrange("p j (c i) -> p c j i", i=4),
+                )
 
         def il_d(key, src, dv):
             if dv > 0:
-                nc.vector.tensor_copy(out=ils[key][:, 0:dv, :], in_=src[:, :, 0:dv].rearrange("p j c -> p c j"))
+                nc.vector.tensor_copy(
+                    out=ils[key][:, 0:dv, :].rearrange("p (c i) j -> p c j i", i=4),
+                    in_=src[:, :, 0:dv].rearrange("p j (c i) -> p c j i", i=4),
+                )
 
         def quant(key, cod, sca, fmt):
             il = ils.pop(key)
@@ -284,16 +302,18 @@ def tile_rdecommunicationlstm_pa_v_kernel(
                 k1[(hc, s)] = (cod, sca)
             quant((n, s), cod, sca, E5)
 
-        def mt(n, i):
+        def mt(n, i, parts=(0, 1), spare=False):
             if not ok(n) or n < 4:
                 return
             hc = n % 4
             s, m = 1 - i // 4, i % 4
-            if n == NSTEP - 1 and i % 2 == 1:
-                o1 = ps_tp.tile([P, IN], F32, name="tpb", tag="tpb")
-            else:
-                o1 = ps_o1.tile([P, IN], F32, name="o1", tag="o1")
-            for gg in (0, 1):
+            if parts[0] == 0:
+                if spare:
+                    o1s[(n, i)] = ps_tp.tile([P, IN], F32, name="tpb", tag="tpb")
+                else:
+                    o1s[(n, i)] = ps_o1.tile([P, IN], F32, name="o1", tag="o1")
+            o1 = o1s[(n, i)]
+            for gg in parts:
                 kc, ks = (k0 if gg == 0 else k1)[(hc, s)]
                 xc, xs = opnd[("x", gg, 0)]
                 nc.tensor.matmul_mx(
@@ -305,7 +325,6 @@ def tile_rdecommunicationlstm_pa_v_kernel(
                     start=(gg == 0),
                     stop=(gg == 1),
                 )
-            o1s[(n, i)] = o1
 
         def eo(n, i, eng=0):
             if not ok(n) or n < 4:
@@ -333,7 +352,8 @@ def tile_rdecommunicationlstm_pa_v_kernel(
         c0row = keep.tile([P, HID], BF16, name="c0row", tag="c0row")
         nc.vector.memset(c0row[:], 0.0)
         nc.sync.dma_start(out=c0row[0:1, :], in_=c_init.rearrange("(o n) -> o n", o=1))
-        ld(0)
+        ld(0, j0=0, j1=2)
+        ld(0, j0=2, j1=4)
         warm = keep.tile([P, 1], F32, name="warm", tag="warm")
         nc.gpsimd.memset(warm[:], 0.0)
         nc.scalar.activation(out=warm[:], in_=warm[:], func=AF.Tanh)
@@ -350,16 +370,29 @@ def tile_rdecommunicationlstm_pa_v_kernel(
         ld(2)
         ld_jobs(0)
 
-        for k in range(-2, NSTEP - 1):
-            if k >= 0:
-                ld(k + 3, (GF, GOUT))
+        for h in (0, 2):
+            for i in range(4):
+                s1(0, i, h, h + 2)
+        chain_a(0, j0=0, j1=2)
+        chain_a(0, j0=2, j1=4)
+        for i in range(4):
+            s1(1, i)
+        for i in range(3):
+            s3(0, i)
+
+        for k in range(0, NSTEP - 1):
+            ld(k + 3, (GF, GOUT))
             ef(k - 1, 1)
             tr(k - 1, 0)
             ita(k - 1, 1)
             ita(k - 1, 0)
             itd(k - 1, 1)
             itd(k - 1, 0)
-            chain_a(k + 1)
+            chain_a(k + 1, (0, 1, 2, 3))
+            chain_b(k, (0,))
+            chain_a(k + 1, (4, 5))
+            if k == 1:
+                jobs_q(0)
             ef(k - 1, 0)
             s1(k + 2, 0)
             s1(k + 2, 1)
@@ -367,7 +400,7 @@ def tile_rdecommunicationlstm_pa_v_kernel(
             qt(k - 1, 0)
             mt(k - 1, 0)
             mt(k - 1, 1)
-            chain_b(k)
+            chain_b(k, (1, 2, 3, 4, 5, 6))
             s1(k + 2, 2)
             eo(k - 1, 0)
             mt(k - 1, 2)
@@ -375,26 +408,22 @@ def tile_rdecommunicationlstm_pa_v_kernel(
             eo(k - 1, 1)
             mt(k - 1, 3)
             if k == 5:
-                e0(0, 0, 0)
-                e0(0, 1, 0)
-                e0(0, 2, 0)
-                e0(0, 3, 0)
+                for j in range(J):
+                    e0(0, j, 0)
             eo(k - 1, 2)
             mt(k - 1, 4)
-            if k >= 0:
-                ld(k + 3, (GO,))
-            jobs_a(k)
+            ld(k + 3, (GO,))
             s3(k + 1, 0)
             eo(k - 1, 3)
             mt(k - 1, 5)
             s3(k + 1, 1)
             eo(k - 1, 4)
             mt(k - 1, 6)
+            jobs_a(k)
             s3(k + 1, 2)
             eo(k - 1, 5)
             mt(k - 1, 7)
-            if k >= 0:
-                ld(k + 3, (GI, GG))
+            ld(k + 3, (GI, GG))
             eo(k - 1, 6)
             eo(k - 1, 7)
             tr(k, 1)
@@ -403,62 +432,77 @@ def tile_rdecommunicationlstm_pa_v_kernel(
             qf_(k - 1, 0)
             mf(k - 1, 1)
             mf(k - 1, 0)
-            jobs_q(k)
-            if k >= 0:
-                ld_jobs(k + 1)
+            if k > 0:
+                jobs_q(k)
+            ld_jobs(k + 1)
 
         ef(6, 1)
+        mt(6, 0, (0,))
+        mt(6, 1, (0,))
         tr(6, 0)
         ita(6, 1)
         ita(6, 0)
         itd(6, 1)
         itd(6, 0)
-        chain_b(7, (0, 1, 2, 3))
-        qt(6, 1)
-        mt(6, 0)
-        mt(6, 1)
-        chain_b(7, (5,))
-        ef(6, 0)
-        tr(7, 1)
+        chain_b(7, (0,))
         qf_(6, 1)
         mf(6, 1)
-        chain_b(7, (4,))
+        chain_b(7, (1,))
+        qt(6, 1)
+        mt(6, 0, (1,))
+        mt(6, 1, (1,))
+        chain_b(7, (2,))
+        ef(6, 0)
         qt(6, 0)
         eo(6, 0)
         mt(6, 2)
+        qf_(6, 0)
         eo(6, 1)
         mt(6, 3)
-        ef(7, 1)
-        ita(7, 1)
-        itd(7, 1)
-        chain_b(7, (6,))
-        tr(7, 0)
-        qf_(7, 1)
-        qt(7, 1)
-        mf(7, 1)
+        mf(6, 0)
+        chain_b(7, (3, 4, 5))
         eo(6, 2)
         mt(6, 4)
         eo(6, 3)
         mt(6, 5)
-        qf_(6, 0)
-        mf(6, 0)
-        ef(7, 0, (0, 1))
-        ita(7, 0)
-        itd(7, 0)
+        tr(7, 1)
+        chain_b(7, (6,))
         eo(6, 4)
         mt(6, 6)
-        eo(6, 5)
+        ef(7, 1, (0, 1))
+        tr(7, 0)
+        eo(6, 5, 1)
         mt(6, 7)
-        qf_(7, 0)
-        qt(7, 0)
-        mf(7, 0)
+        ita(7, 1)
+        itd(7, 1)
         eo(6, 6, 0)
+        qf_(7, 1)
+        mf(7, 1)
+        ef(7, 0, (0, 1))
+        qt(7, 1)
+        mt(7, 0, (0, 1), True)
+        mt(7, 1, (0, 1), True)
+        ita(7, 0)
+        itd(7, 0)
         eo(6, 7, 0)
-        for i in range(4):
-            mt(7, i)
-        for j in range(J):
-            e0(1, j, 1 - j % 2)
-        for i in range(8):
-            eo(7, i, i % 2)
-            if i + 4 < 8:
-                mt(7, i + 4)
+        mt(7, 2)
+        mt(7, 3)
+        qf_(7, 0)
+        mf(7, 0)
+        qt(7, 0)
+        eo(7, 0, 0)
+        mt(7, 4, (0, 1), True)
+        eo(7, 1, 0)
+        mt(7, 5, (0, 1), True)
+        eo(7, 2, 1)
+        mt(7, 6)
+        eo(7, 3, 0)
+        mt(7, 7)
+        e0(1, 0, 1)
+        e0(1, 1, 0)
+        e0(1, 2, 1)
+        e0(1, 3, 0)
+        eo(7, 4, 1)
+        eo(7, 5, 0)
+        eo(7, 6, 1)
+        eo(7, 7, 0)

@@ -22,8 +22,8 @@ WC = 256
 NSTEP = 8
 GI, GF, GG, GO = 0, 1, 2, 3
 GOUT = 4
+S1_ORDER = (GI, GG, GF, GO)
 
-DV_IT = (32, 32, 32, 32, 160, 160, 224, 336)
 JOBS = {
     0: (("w", 0, 1), ("w", 0, 0)),
     1: (("w", 1, 1), ("w", 1, 0)),
@@ -31,7 +31,7 @@ JOBS = {
     3: (("w", 3, 1), ("w", 3, 0)),
     4: (("x", 0, 0), ("x", 1, 0)),
 }
-DV_JOB = {0: 0, 1: 96, 2: 128, 3: 128, 4: 128}
+DV_JOB = {0: 0, 1: 0, 2: 0, 3: 0, 4: 0}
 
 
 def tile_rdecommunicationlstm_pa_v_kernel(
@@ -46,11 +46,14 @@ def tile_rdecommunicationlstm_pa_v_kernel(
     out1_v = out_1.rearrange("(t m) n -> t m n", m=P)
 
     with ExitStack() as ctx:
-        zp = ctx.enter_context(tc.tile_pool(name="zp", bufs=3))
+        zrp = ctx.enter_context(tc.tile_pool(name="zrp", bufs=1))
+        gop = ctx.enter_context(tc.tile_pool(name="gop", bufs=2))
+        avp = ctx.enter_context(tc.tile_pool(name="avp", bufs=3))
+        afp = ctx.enter_context(tc.tile_pool(name="afp", bufs=2))
         tp = ctx.enter_context(tc.tile_pool(name="tp", bufs=2))
         dzp = ctx.enter_context(tc.tile_pool(name="dzp", bufs=2))
-        ilp = ctx.enter_context(tc.tile_pool(name="ilp", bufs=4))
-        rawp = ctx.enter_context(tc.tile_pool(name="rawp", bufs=3))
+        ilp = ctx.enter_context(tc.tile_pool(name="ilp", bufs=2))
+        rawp = ctx.enter_context(tc.tile_pool(name="rawp", bufs=2))
         keep = ctx.enter_context(tc.tile_pool(name="keep", bufs=1))
         k1p = ctx.enter_context(tc.tile_pool(name="k1p", bufs=4))
         qfp = ctx.enter_context(tc.tile_pool(name="qfp", bufs=4))
@@ -61,7 +64,8 @@ def tile_rdecommunicationlstm_pa_v_kernel(
         ps_o1 = ctx.enter_context(tc.psum_pool(name="ps_o1", bufs=2))
         ctx.enter_context(tc.manual_schedule())
 
-        zt = {}
+        zr = {}
+        av = {}
         tt = {}
         dzt = {}
         raws = {}
@@ -84,23 +88,27 @@ def tile_rdecommunicationlstm_pa_v_kernel(
             else:
                 nc.vector.tensor_copy(out=out, in_=in_)
 
-        def stt(out, in0, scalar, in1, op0=ALU.add):
-            nc.vector.scalar_tensor_tensor(out=out, in0=in0, scalar=scalar, in1=in1, op0=op0, op1=ALU.mult)
+        def stt(out, in0, scalar, in1):
+            nc.vector.scalar_tensor_tensor(out=out, in0=in0, scalar=scalar, in1=in1, op0=ALU.add, op1=ALU.mult)
 
-        def ld(n, which=(GI, GG, GF, GO, GOUT), j0=0, j1=J):
+        def mul(out, in0, in1):
+            nc.vector.tensor_tensor(out=out, in0=in0, in1=in1, op=ALU.mult)
+
+        def ld(n, gt, a0=0, a1=2):
             if not ok(n):
                 return
             g, hc = n // 4, n % 4
-            tl = zt.get(n, {})
-            for gt in which:
-                if gt not in tl:
-                    tl[gt] = zp.tile([P, J, WC], BF16 if gt == GOUT else F32, name="z%d" % gt, tag="z%d" % gt)
+            if (n, gt) not in zr:
                 if gt == GOUT:
-                    nc.sync.dma_start(out=tl[gt][:, j0:j1, :], in_=go_v[g, :, j0:j1, hc * WC:(hc + 1) * WC])
+                    zr[(n, gt)] = gop.tile([P, J, WC], BF16, name="go", tag="go")
                 else:
-                    c0 = gt * HID + hc * WC
-                    nc.sync.dma_start(out=tl[gt][:, j0:j1, :], in_=gates_v[g, :, j0:j1, c0:c0 + WC])
-            zt[n] = tl
+                    zr[(n, gt)] = zrp.tile([P, J, WC], F32, name="z%d" % gt, tag="z%d" % gt)
+            t = zr[(n, gt)]
+            if gt == GOUT:
+                nc.sync.dma_start(out=t[:, 2 * a0:2 * a1, :], in_=go_v[g, :, 2 * a0:2 * a1, hc * WC:(hc + 1) * WC])
+            else:
+                c0 = gt * HID + hc * WC
+                nc.sync.dma_start(out=t[:, 2 * a0:2 * a1, :], in_=gates_v[g, :, 2 * a0:2 * a1, c0:c0 + WC])
 
         def ld_jobs(k):
             for job in JOBS.get(k, ()):
@@ -112,36 +120,41 @@ def tile_rdecommunicationlstm_pa_v_kernel(
                     nc.sync.dma_start(out=t[:], in_=x_v[job[1]])
                 raws[job] = t
 
-        def s1(n, i, j0=0, j1=J):
+        def s1(n, i, a0=0, a1=2):
             if not ok(n):
                 return
-            gt = ((GI, GG, GF, GO) if n < 3 else (GF, GO, GI, GG))[i]
-            t = zt[n][gt][:, j0:j1, :]
-            nc.scalar.activation(out=t, in_=t, func=AF.Tanh, scale=(1.0 if gt == GG else 0.5))
+            gt = S1_ORDER[i]
+            if (n, gt) not in av:
+                pool = afp if gt == GF else avp
+                av[(n, gt)] = pool.tile([P, 2, WC, 2], F32, name="a%d" % gt, tag="a%d" % gt)
+            nc.scalar.activation(
+                out=av[(n, gt)][:, a0:a1, :, :],
+                in_=zr[(n, gt)][:, 2 * a0:2 * a1, :].rearrange("p (a e) c -> p a c e", e=2),
+                func=(AF.Tanh if gt == GG else AF.Sigmoid),
+            )
 
-        def chain_a(n, which=(0, 1, 2, 3, 4, 5), j0=0, j1=J):
+        def chain_a(n, which=(0, 1, 2, 3, 4, 5), a0=0, a1=2):
             if not ok(n):
                 return
             hc = n % 4
             if n not in tt:
                 tn = {}
                 for i in range(1, 6):
-                    tn[i] = tp.tile([P, J, WC], F32, name="t%d" % i, tag="t%d" % i)
+                    tn[i] = tp.tile([P, 2, WC, 2], F32, name="t%d" % i, tag="t%d" % i)
                 tt[n] = tn
             t = {}
             for i in range(1, 6):
-                t[i] = tt[n][i][:, j0:j1, :]
+                t[i] = tt[n][i][:, a0:a1, :, :]
             z = {}
-            for gt in (GI, GF, GG, GO, GOUT):
-                z[gt] = zt[n][gt][:, j0:j1, :]
-            c0s = c0b[:, hc * WC:(hc + 1) * WC].unsqueeze(1).to_broadcast([P, j1 - j0, WC])
+            for gt in (GI, GF, GG, GO):
+                z[gt] = av[(n, gt)][:, a0:a1, :, :]
             for i in which:
                 if i == 0:
-                    stt(t[1], z[GI], 1.0, z[GG])
+                    mul(t[1], z[GI], z[GG])
                 elif i == 1:
-                    stt(t[2], z[GF], 1.0, c0s)
+                    mul(t[2], z[GF], c0d[:, hc * WC:(hc + 1) * WC, :].unsqueeze(1).to_broadcast([P, a1 - a0, WC, 2]))
                 elif i == 2:
-                    stt(t[5], z[GO], 1.0, z[GOUT])
+                    mul(t[5], z[GO], zr[(n, GOUT)][:, 2 * a0:2 * a1, :].rearrange("p (a e) c -> p a c e", e=2))
                 elif i == 3:
                     nc.vector.tensor_tensor(out=t[3], in0=t[1], in1=t[2], op=ALU.add)
                 elif i == 4:
@@ -153,52 +166,56 @@ def tile_rdecommunicationlstm_pa_v_kernel(
             if not ok(n):
                 return
             t = tt[n]
-            gg = zt[n][GG]
+            gg = av[(n, GG)]
             if part == 0:
-                nc.scalar.activation(out=gg[:], in_=gg[:], func=AF.Square, scale=0.5)
+                nc.scalar.activation(out=gg[:], in_=gg[:], func=AF.Square)
             elif part == 1:
-                nc.scalar.activation(out=t[3][:], in_=t[3][:], func=AF.Tanh, scale=0.5)
+                nc.scalar.activation(out=t[3][:], in_=t[3][:], func=AF.Tanh, scale=-1.0)
             else:
                 nc.scalar.activation(out=t[4][:], in_=t[3][:], func=AF.Square)
+
+        def last(dz, lo, in0, in1):
+            mul(
+                dz[:, lo:lo + WC, :].rearrange("p c (a e) -> p c a e", e=2),
+                in0[:].rearrange("p a c e -> p c a e"),
+                in1[:].rearrange("p a c e -> p c a e"),
+            )
 
         def chain_b(n, which=(0, 1, 2, 3, 4, 5, 6)):
             if not ok(n):
                 return
-            tl = zt[n]
             t = tt[n]
+            ai, gg, ao = av[(n, GI)], av[(n, GG)], av[(n, GO)]
             if which[0] == 0:
-                dz0 = dzp.tile([P, J, 2 * WC], BF16, name="dz0", tag="dz0")
-                dz1 = dzp.tile([P, J, 2 * WC], BF16, name="dz1", tag="dz1")
+                dz0 = dzp.tile([P, 2 * WC, J], BF16, name="dz0", tag="dz0", align_bytes=64)
+                dz1 = dzp.tile([P, 2 * WC, J], BF16, name="dz1", tag="dz1", align_bytes=64)
                 dzt[n] = (dz0, dz1)
             dz0, dz1 = dzt[n]
             for i in which:
                 if i == 0:
-                    stt(tl[GO][:], tl[GO][:], -1.0, t[3][:])
+                    stt(ao[:], ao[:], -1.0, t[3][:])
                 elif i == 1:
                     stt(t[4][:], t[4][:], -1.0, t[5][:])
                 elif i == 2:
-                    stt(dz1[:, :, WC:2 * WC], tl[GO][:], -0.25, t[5][:], op0=ALU.mult)
+                    last(dz1, WC, ao, t[5])
                 elif i == 3:
-                    stt(tl[GI][:], tl[GI][:], 1.0, t[4][:])
+                    stt(gg[:], gg[:], -1.0, ai[:])
                 elif i == 4:
-                    stt(dz0[:, :, 0:WC], t[1][:], 0.125, t[4][:], op0=ALU.mult)
+                    last(dz0, 0, t[1], t[4])
                 elif i == 5:
-                    stt(dz1[:, :, 0:WC], tl[GG][:], -0.25, tl[GI][:])
+                    last(dz1, 0, gg, t[4])
                 else:
-                    stt(dz0[:, :, WC:2 * WC], t[2][:], 0.125, t[4][:], op0=ALU.mult)
+                    last(dz0, WC, t[2], t[4])
 
         def tr(n, s):
             if not ok(n):
                 return
-            dz = dzt[n][s]
+            words = dzt[n][s][:].rearrange("p c j -> p (c j)").bitcast(F32)
             bl = []
-            for b in (0, 1):
+            for a in (0, 1):
                 bank = ps_tp.tile([P, 4 * P], F32, name="tpb", tag="tpb")
-                for jj in (0, 1):
-                    words = dz[:, 2 * b + jj, :].bitcast(F32)
-                    for u in (0, 1):
-                        k = 2 * jj + u
-                        nc.tensor.transpose(bank[:, k * P:(k + 1) * P], words[:, u:256:2], ident[:])
+                for t in range(4):
+                    nc.tensor.transpose(bank[:, t * P:(t + 1) * P], words[:, 2 * t + a:4 * WC:8], ident[:])
                 bl.append(bank)
             banks[(n, s)] = bl
 
@@ -207,12 +224,12 @@ def tile_rdecommunicationlstm_pa_v_kernel(
                 return
             bl = banks.pop((n, s))
             ql = []
-            for b in (0, 1):
+            for a in (0, 1):
                 qf = qfp.tile([P, 8 * P], BF16, name="qf", tag="qf", align_bytes=64)
                 copy_on(
-                    engs[b],
-                    qf[:].bitcast(F32).rearrange("p (b r u) -> p b r u", b=2, u=2),
-                    bl[b][:].rearrange("p (b u r) -> p b r u", b=2, u=2),
+                    engs[a],
+                    qf[:].rearrange("p (e r t) -> p e r t", e=2, t=4),
+                    bl[a][:].bitcast(BF16).rearrange("p (t r e) -> p e r t", t=4, e=2),
                 )
                 ql.append(qf)
             qfs[(n, s)] = ql
@@ -222,10 +239,10 @@ def tile_rdecommunicationlstm_pa_v_kernel(
                 return
             ql = qfs.pop((n, s))
             fl = []
-            for b in (0, 1):
+            for a in (0, 1):
                 fc = fcp.tile([P, 2 * P], U32, name="fc", tag="fc", align_bytes=64)
                 fs = fcp.tile([P, 2 * P], U8, name="fs", tag="fs", align_bytes=64)
-                nc.vector.quantize_mx(out=fc[:].bitcast(E5), scales=fs[:], in_=ql[b][:])
+                nc.vector.quantize_mx(out=fc[:].bitcast(E5), scales=fs[:], in_=ql[a][:])
                 fl.append((fc, fs))
             fcs[(n, s)] = fl
 
@@ -238,13 +255,13 @@ def tile_rdecommunicationlstm_pa_v_kernel(
                     acc[j] = ps_acc.tile([P, IN], F32, name="acc%d" % j, tag="acc%d" % j)
             fl = fcs.pop((n, s))
             wc, ws = opnd[("w", hc, s)]
-            for b in (0, 1):
-                fc, fs = fl[b]
-                for jj in (0, 1):
+            for a in (0, 1):
+                fc, fs = fl[a]
+                for e in (0, 1):
                     nc.tensor.matmul_mx(
-                        out=acc[2 * b + jj][:],
-                        lhsT=fc[:, jj * P:(jj + 1) * P].bitcast(E5),
-                        lhsT_scale=fs[:, jj * P:(jj + 1) * P],
+                        out=acc[2 * a + e][:],
+                        lhsT=fc[:, e * P:(e + 1) * P].bitcast(E5),
+                        lhsT_scale=fs[:, e * P:(e + 1) * P],
                         rhs=wc[:].bitcast(E4),
                         rhs_scale=ws[:],
                         start=(hc == 0 and s == 1),
@@ -259,34 +276,6 @@ def tile_rdecommunicationlstm_pa_v_kernel(
         def e0(g, j, eng):
             store(out0_v[g, j], acc[j], eng)
 
-        def il_a(key, src, dv):
-            il = ilp.tile([P, IN, J], BF16, name="il", tag="il", align_bytes=64)
-            ils[key] = il
-            if dv < IN:
-                nc.scalar.copy(
-                    out=il[:, dv:IN, :].rearrange("p (c i) j -> p c j i", i=4),
-                    in_=src[:, :, dv:IN].rearrange("p j (c i) -> p c j i", i=4),
-                )
-
-        def il_d(key, src, dv):
-            if dv > 0:
-                nc.vector.tensor_copy(
-                    out=ils[key][:, 0:dv, :].rearrange("p (c i) j -> p c j i", i=4),
-                    in_=src[:, :, 0:dv].rearrange("p j (c i) -> p c j i", i=4),
-                )
-
-        def quant(key, cod, sca, fmt):
-            il = ils.pop(key)
-            nc.vector.quantize_mx(out=cod[:].bitcast(fmt), scales=sca[:], in_=il[:].rearrange("p c j -> p (c j)"))
-
-        def ita(n, s):
-            if ok(n):
-                il_a((n, s), dzt[n][s], DV_IT[n])
-
-        def itd(n, s):
-            if ok(n):
-                il_d((n, s), dzt[n][s], DV_IT[n])
-
         def qt(n, s):
             if not ok(n):
                 return
@@ -300,7 +289,7 @@ def tile_rdecommunicationlstm_pa_v_kernel(
                 cod = k1p.tile([P, IN], U32, name="k1c", tag="k1c", align_bytes=64)
                 sca = k1p.tile([P, IN], U8, name="k1s", tag="k1s", align_bytes=64)
                 k1[(hc, s)] = (cod, sca)
-            quant((n, s), cod, sca, E5)
+            nc.vector.quantize_mx(out=cod[:].bitcast(E5), scales=sca[:], in_=dzt[n][s][:].rearrange("p c j -> p (c j)"))
 
         def mt(n, i, parts=(0, 1), spare=False):
             if not ok(n) or n < 4:
@@ -334,97 +323,109 @@ def tile_rdecommunicationlstm_pa_v_kernel(
             store(out1_v[(2 * s + m // 2) * 8 + hc * 2 + m % 2], o1s.pop((n, i)), eng)
 
         def jobs_a(k):
+            dv = DV_JOB.get(k, 0)
             for job in JOBS.get(k, ()):
-                il_a(job, raws[job], DV_JOB[k])
+                il = ilp.tile([P, IN, J], BF16, name="il", tag="il", align_bytes=64)
+                ils[job] = il
+                nc.scalar.copy(
+                    out=il[:, dv:IN, :].rearrange("p (c i) j -> p c j i", i=4),
+                    in_=raws[job][:, :, dv:IN].rearrange("p j (c i) -> p c j i", i=4),
+                )
 
         def jobs_d(k):
+            dv = DV_JOB.get(k, 0)
             for job in JOBS.get(k, ()):
-                il_d(job, raws.pop(job), DV_JOB[k])
+                if dv > 0:
+                    nc.vector.tensor_copy(
+                        out=ils[job][:, 0:dv, :].rearrange("p (c i) j -> p c j i", i=4),
+                        in_=raws[job][:, :, 0:dv].rearrange("p j (c i) -> p c j i", i=4),
+                    )
 
         def jobs_q(k):
             for job in JOBS.get(k, ()):
                 nm = "%s%d%d" % job
                 cod = keep.tile([P, IN], U32, name="c" + nm, tag="c" + nm, align_bytes=64)
                 sca = keep.tile([P, IN], U8, name="s" + nm, tag="s" + nm, align_bytes=64)
-                quant(job, cod, sca, E4)
+                nc.vector.quantize_mx(out=cod[:].bitcast(E4), scales=sca[:], in_=ils.pop(job)[:].rearrange("p c j -> p (c j)"))
                 opnd[job] = (cod, sca)
 
         c0row = keep.tile([P, HID], BF16, name="c0row", tag="c0row")
         nc.vector.memset(c0row[:], 0.0)
         nc.sync.dma_start(out=c0row[0:1, :], in_=c_init.rearrange("(o n) -> o n", o=1))
-        ld(0, j0=0, j1=2)
-        ld(0, j0=2, j1=4)
+        for a in (0, 1):
+            for gt in (GI, GG, GF, GO, GOUT):
+                ld(0, gt, a, a + 1)
         warm = keep.tile([P, 1], F32, name="warm", tag="warm")
         nc.gpsimd.memset(warm[:], 0.0)
-        nc.scalar.activation(out=warm[:], in_=warm[:], func=AF.Tanh)
+        nc.scalar.activation(out=warm[:], in_=warm[:], func=AF.Sigmoid)
         ones = keep.tile([P, P], BF16, name="ones", tag="ones")
         nc.vector.memset(ones[:], 1.0)
         ident = keep.tile([P, P], F32, name="ident", tag="ident")
         masks.make_identity(nc, ident[:])
-        c0b = keep.tile([P, HID], BF16, name="c0b", tag="c0b")
+        c0d = keep.tile([P, HID, 2], BF16, name="c0d", tag="c0d")
         for h in (0, 1):
             bank = ps_tp.tile([P, 4 * P], F32, name="tpb", tag="tpb")
             nc.tensor.matmul(bank[:], lhsT=ones[:], rhs=c0row[:, h * 512:(h + 1) * 512], start=True, stop=True)
-            nc.vector.tensor_copy(out=c0b[:, h * 512:(h + 1) * 512], in_=bank[:])
-        ld(1)
-        ld(2)
-        ld_jobs(0)
-
-        for h in (0, 2):
+            nc.vector.tensor_copy(out=c0d[:, h * 512:(h + 1) * 512, :], in_=bank[:].unsqueeze(2).to_broadcast([P, 512, 2]))
+        ld(1, GOUT)
+        for a in (0, 1):
             for i in range(4):
-                s1(0, i, h, h + 2)
-        chain_a(0, j0=0, j1=2)
-        chain_a(0, j0=2, j1=4)
+                s1(0, i, a, a + 1)
+                if a == 1:
+                    ld(1, S1_ORDER[i])
+        chain_a(0, a0=0, a1=1)
+        chain_a(0, a0=1, a1=2)
+        ld(2, GOUT)
         for i in range(4):
             s1(1, i)
+            ld(2, S1_ORDER[i])
+        ld_jobs(0)
         for i in range(3):
             s3(0, i)
 
         for k in range(0, NSTEP - 1):
-            ld(k + 3, (GF, GOUT))
             ef(k - 1, 1)
             tr(k - 1, 0)
-            ita(k - 1, 1)
-            ita(k - 1, 0)
-            itd(k - 1, 1)
-            itd(k - 1, 0)
-            chain_a(k + 1, (0, 1, 2, 3))
-            chain_b(k, (0,))
-            chain_a(k + 1, (4, 5))
-            if k == 1:
-                jobs_q(0)
-            ef(k - 1, 0)
-            s1(k + 2, 0)
-            s1(k + 2, 1)
             qt(k - 1, 1)
             qt(k - 1, 0)
             mt(k - 1, 0)
             mt(k - 1, 1)
-            chain_b(k, (1, 2, 3, 4, 5, 6))
-            s1(k + 2, 2)
+            chain_a(k + 1, (0, 1, 2, 3))
+            ld(k + 3, GOUT)
+            chain_b(k, (0,))
+            chain_a(k + 1, (4, 5))
+            if 1 <= k <= 4:
+                jobs_q(k - 1)
+            s1(k + 2, 0)
+            ld(k + 3, S1_ORDER[0])
             eo(k - 1, 0)
             mt(k - 1, 2)
-            s1(k + 2, 3)
+            s1(k + 2, 1)
+            ld(k + 3, S1_ORDER[1])
             eo(k - 1, 1)
             mt(k - 1, 3)
+            ef(k - 1, 0)
+            chain_b(k, (1, 2, 3, 4, 5, 6))
+            eo(k - 1, 2)
+            mt(k - 1, 4)
+            s1(k + 2, 2)
+            ld(k + 3, S1_ORDER[2])
+            eo(k - 1, 3)
+            mt(k - 1, 5)
+            s1(k + 2, 3)
+            ld(k + 3, S1_ORDER[3])
             if k == 5:
                 for j in range(J):
                     e0(0, j, 0)
-            eo(k - 1, 2)
-            mt(k - 1, 4)
-            ld(k + 3, (GO,))
-            s3(k + 1, 0)
-            eo(k - 1, 3)
-            mt(k - 1, 5)
-            s3(k + 1, 1)
             eo(k - 1, 4)
             mt(k - 1, 6)
-            jobs_a(k)
-            s3(k + 1, 2)
+            s3(k + 1, 0)
             eo(k - 1, 5)
             mt(k - 1, 7)
-            ld(k + 3, (GI, GG))
+            s3(k + 1, 1)
             eo(k - 1, 6)
+            jobs_a(k)
+            s3(k + 1, 2)
             eo(k - 1, 7)
             tr(k, 1)
             jobs_d(k)
@@ -432,77 +433,67 @@ def tile_rdecommunicationlstm_pa_v_kernel(
             qf_(k - 1, 0)
             mf(k - 1, 1)
             mf(k - 1, 0)
-            if k > 0:
+            if k == 4:
                 jobs_q(k)
             ld_jobs(k + 1)
 
         ef(6, 1)
-        mt(6, 0, (0,))
-        mt(6, 1, (0,))
-        tr(6, 0)
-        ita(6, 1)
-        ita(6, 0)
-        itd(6, 1)
-        itd(6, 0)
-        chain_b(7, (0,))
-        qf_(6, 1)
-        mf(6, 1)
-        chain_b(7, (1,))
         qt(6, 1)
-        mt(6, 0, (1,))
-        mt(6, 1, (1,))
-        chain_b(7, (2,))
-        ef(6, 0)
         qt(6, 0)
+        mt(6, 0)
+        mt(6, 1)
+        tr(6, 0)
+        chain_b(7, (0, 1))
         eo(6, 0)
         mt(6, 2)
-        qf_(6, 0)
         eo(6, 1)
         mt(6, 3)
-        mf(6, 0)
-        chain_b(7, (3, 4, 5))
+        qf_(6, 1)
+        mf(6, 1)
+        chain_b(7, (2, 3))
+        ef(6, 0)
         eo(6, 2)
         mt(6, 4)
         eo(6, 3)
         mt(6, 5)
+        chain_b(7, (5,))
         tr(7, 1)
-        chain_b(7, (6,))
+        qf_(6, 0)
+        mf(6, 0)
+        chain_b(7, (4,))
         eo(6, 4)
         mt(6, 6)
+        eo(6, 5)
+        mt(6, 7)
+        qt(7, 1)
+        chain_b(7, (6,))
         ef(7, 1, (0, 1))
         tr(7, 0)
-        eo(6, 5, 1)
-        mt(6, 7)
-        ita(7, 1)
-        itd(7, 1)
         eo(6, 6, 0)
+        mt(7, 0)
+        eo(6, 7, 0)
+        mt(7, 1)
         qf_(7, 1)
         mf(7, 1)
+        qt(7, 0)
         ef(7, 0, (0, 1))
-        qt(7, 1)
-        mt(7, 0, (0, 1), True)
-        mt(7, 1, (0, 1), True)
-        ita(7, 0)
-        itd(7, 0)
-        eo(6, 7, 0)
-        mt(7, 2)
-        mt(7, 3)
+        mt(7, 2, (0, 1), True)
+        mt(7, 3, (0, 1), True)
         qf_(7, 0)
         mf(7, 0)
-        qt(7, 0)
         eo(7, 0, 0)
-        mt(7, 4, (0, 1), True)
-        eo(7, 1, 0)
-        mt(7, 5, (0, 1), True)
-        eo(7, 2, 1)
-        mt(7, 6)
-        eo(7, 3, 0)
-        mt(7, 7)
-        e0(1, 0, 1)
-        e0(1, 1, 0)
-        e0(1, 2, 1)
-        e0(1, 3, 0)
-        eo(7, 4, 1)
-        eo(7, 5, 0)
-        eo(7, 6, 1)
-        eo(7, 7, 0)
+        mt(7, 4)
+        eo(7, 1, 1)
+        mt(7, 5)
+        eo(7, 2, 0)
+        mt(7, 6, (0, 1), True)
+        eo(7, 3, 1)
+        mt(7, 7, (0, 1), True)
+        e0(1, 0, 0)
+        e0(1, 1, 1)
+        e0(1, 2, 0)
+        e0(1, 3, 1)
+        eo(7, 4, 0)
+        eo(7, 5, 1)
+        eo(7, 6, 0)
+        eo(7, 7, 1)

@@ -152,7 +152,7 @@ def tile_rdecommunicationlstm_pa_v_kernel(
                 if i == 0:
                     mul(t[1], z[GI], z[GG])
                 elif i == 1:
-                    mul(t[2], z[GF], c0d[:, hc * WC:(hc + 1) * WC, :].unsqueeze(1).to_broadcast([P, a1 - a0, WC, 2]))
+                    mul(t[2], z[GF], c0b[:, hc * WC:(hc + 1) * WC].unsqueeze(1).unsqueeze(3).to_broadcast([P, a1 - a0, WC, 2]))
                 elif i == 2:
                     mul(t[5], z[GO], zr[(n, GOUT)][:, 2 * a0:2 * a1, :].rearrange("p (a e) c -> p a c e", e=2))
                 elif i == 3:
@@ -351,10 +351,13 @@ def tile_rdecommunicationlstm_pa_v_kernel(
 
         c0row = keep.tile([P, HID], BF16, name="c0row", tag="c0row")
         nc.vector.memset(c0row[:], 0.0)
+        ld(0, GI, 0, 1)
+        ld(0, GG, 0, 1)
         nc.sync.dma_start(out=c0row[0:1, :], in_=c_init.rearrange("(o n) -> o n", o=1))
-        for a in (0, 1):
-            for gt in (GI, GG, GF, GO, GOUT):
-                ld(0, gt, a, a + 1)
+        for gt in (GF, GO, GOUT):
+            ld(0, gt, 0, 1)
+        for gt in (GI, GG, GF, GO, GOUT):
+            ld(0, gt, 1, 2)
         warm = keep.tile([P, 1], F32, name="warm", tag="warm")
         nc.gpsimd.memset(warm[:], 0.0)
         nc.scalar.activation(out=warm[:], in_=warm[:], func=AF.Sigmoid)
@@ -362,23 +365,35 @@ def tile_rdecommunicationlstm_pa_v_kernel(
         nc.vector.memset(ones[:], 1.0)
         ident = keep.tile([P, P], F32, name="ident", tag="ident")
         masks.make_identity(nc, ident[:])
-        c0d = keep.tile([P, HID, 2], BF16, name="c0d", tag="c0d")
+        c0b = keep.tile([P, HID], BF16, name="c0b", tag="c0b")
+        c0ps = []
         for h in (0, 1):
             bank = ps_tp.tile([P, 4 * P], F32, name="tpb", tag="tpb")
             nc.tensor.matmul(bank[:], lhsT=ones[:], rhs=c0row[:, h * 512:(h + 1) * 512], start=True, stop=True)
-            nc.vector.tensor_copy(out=c0d[:, h * 512:(h + 1) * 512, :], in_=bank[:].unsqueeze(2).to_broadcast([P, 512, 2]))
+            c0ps.append(bank)
+
+        def c0_piece(lo, hi, eng):
+            copy_on(eng, c0b[:, lo:hi], c0ps[lo // 512][:, lo % 512:lo % 512 + hi - lo])
+
+        for i in range(4):
+            lent = tp.tile([P, 2, WC, 2], F32, name="t%d" % (i + 1), tag="t%d" % (i + 1))
+            zr[(1, S1_ORDER[i])] = lent[:].rearrange("p a c e -> p (a c e)").rearrange("p (j c) -> p j c", j=J)
+            ld(1, S1_ORDER[i])
         ld(1, GOUT)
         for a in (0, 1):
             for i in range(4):
                 s1(0, i, a, a + 1)
                 if a == 1:
-                    ld(1, S1_ORDER[i])
-        chain_a(0, a0=0, a1=1)
+                    ld(2, S1_ORDER[i])
+        chain_a(0, (0,), 0, 1)
+        c0_piece(0, WC, 1)
+        chain_a(0, (1, 2, 3, 4, 5), 0, 1)
         chain_a(0, a0=1, a1=2)
         ld(2, GOUT)
+        c0_piece(WC, 512, 0)
+        c0_piece(512, 1024, 0)
         for i in range(4):
             s1(1, i)
-            ld(2, S1_ORDER[i])
         ld_jobs(0)
         for i in range(3):
             s3(0, i)

from contextlib import ExitStack

import concourse.masks as masks
import concourse.mybir as mybir

B, IN, HID, NG = 1024, 512, 1024, 4
FLOPS = 2 * 2 * B * NG * HID * IN
BYTES = 4 * B * NG * HID + 2 * B * HID + 2 * NG * HID * IN + 2 * B * IN + 2 * HID + 4 * B * IN + 4 * NG * HID * IN

F32 = mybir.dt.float32
BF16 = mybir.dt.bfloat16
U32 = mybir.dt.uint32
U8 = mybir.dt.uint8
E4 = mybir.dt.float8_e4m3fn_x4
E5 = mybir.dt.float8_e5m2_x4
AF = mybir.ActivationFunctionType
ALU = mybir.AluOpType

P = 128
J = 4
WC = 256
NSTEP = 8
GI, GF, GG, GO = 0, 1, 2, 3
GOUT = 4
S1_ORDER = (GI, GG, GF, GO)

JOBS = {
    0: (("w", 0, 1), ("w", 0, 0)),
    1: (("w", 1, 1), ("w", 1, 0)),
    2: (("w", 2, 1), ("w", 2, 0)),
    3: (("w", 3, 1), ("w", 3, 0)),
    4: (("x", 0, 0), ("x", 1, 0)),
}
DV_JOB = {0: 0, 1: 0, 2: 0, 3: 0, 4: 0}


def tile_rdecommunicationlstm_pa_v_kernel(
    tc, regime_vector, W_ih0, hh_gates, b_ih0, b_hh0, c_init, gates, grad_out, out_0, out_1
):
    nc = tc.nc
    gates_v = gates.rearrange("(g p j) c -> g p j c", p=P, j=J)
    go_v = grad_out.rearrange("(g p j) h -> g p j h", p=P, j=J)
    w_v = W_ih0.rearrange("(q m j) n -> q m j n", m=64, j=J)
    x_v = regime_vector.rearrange("(g p j) n -> g p j n", p=P, j=J)
    out0_v = out_0.rearrange("(g p j) n -> g j p n", p=P, j=J)
    out1_v = out_1.rearrange("(t m) n -> t m n", m=P)

    with ExitStack() as ctx:
        zrp = ctx.enter_context(tc.tile_pool(name="zrp", bufs=1))
        gop = ctx.enter_context(tc.tile_pool(name="gop", bufs=2))
        avp = ctx.enter_context(tc.tile_pool(name="avp", bufs=3))
        afp = ctx.enter_context(tc.tile_pool(name="afp", bufs=2))
        tp = ctx.enter_context(tc.tile_pool(name="tp", bufs=2))
        dzp = ctx.enter_context(tc.tile_pool(name="dzp", bufs=2))
        ilp = ctx.enter_context(tc.tile_pool(name="ilp", bufs=2))
        rawp = ctx.enter_context(tc.tile_pool(name="rawp", bufs=2))
        keep = ctx.enter_context(tc.tile_pool(name="keep", bufs=1))
        k1p = ctx.enter_context(tc.tile_pool(name="k1p", bufs=4))
        qfp = ctx.enter_context(tc.tile_pool(name="qfp", bufs=4))
        fcp = ctx.enter_context(tc.tile_pool(name="fcp", bufs=4))
        outp = ctx.enter_context(tc.tile_pool(name="outp", bufs=9))
        ps_acc = ctx.enter_context(tc.psum_pool(name="ps_acc", bufs=1))
        ps_tp = ctx.enter_context(tc.psum_pool(name="ps_tp", bufs=2))
        ps_o1 = ctx.enter_context(tc.psum_pool(name="ps_o1", bufs=2))
        ctx.enter_context(tc.manual_schedule())

        zr = {}
        av = {}
        tt = {}
        dzt = {}
        raws = {}
        ils = {}
        opnd = {}
        k0 = {}
        k1 = {}
        acc = {}
        banks = {}
        qfs = {}
        fcs = {}
        o1s = {}

        def ok(n):
            return 0 <= n < NSTEP

        def copy_on(eng, out, in_):
            if eng == 0:
                nc.scalar.copy(out=out, in_=in_)
            else:
                nc.vector.tensor_copy(out=out, in_=in_)

        def stt(out, in0, scalar, in1):
            nc.vector.scalar_tensor_tensor(out=out, in0=in0, scalar=scalar, in1=in1, op0=ALU.add, op1=ALU.mult)

        def mul(out, in0, in1):
            nc.vector.tensor_tensor(out=out, in0=in0, in1=in1, op=ALU.mult)

        def ld(n, gt, a0=0, a1=2):
            if not ok(n):
                return
            g, hc = n // 4, n % 4
            if (n, gt) not in zr:
                if gt == GOUT:
                    zr[(n, gt)] = gop.tile([P, J, WC], BF16, name="go", tag="go")
                else:
                    zr[(n, gt)] = zrp.tile([P, J, WC], F32, name="z%d" % gt, tag="z%d" % gt)
            t = zr[(n, gt)]
            if gt == GOUT:
                nc.sync.dma_start(out=t[:, 2 * a0:2 * a1, :], in_=go_v[g, :, 2 * a0:2 * a1, hc * WC:(hc + 1) * WC])
            else:
                c0 = gt * HID + hc * WC
                nc.sync.dma_start(out=t[:, 2 * a0:2 * a1, :], in_=gates_v[g, :, 2 * a0:2 * a1, c0:c0 + WC])

        def ld_jobs(k):
            for job in JOBS.get(k, ()):
                t = rawp.tile([P, J, IN], BF16, name="raw", tag="raw")
                if job[0] == "w":
                    for hf in (0, 1):
                        nc.sync.dma_start(out=t[64 * hf:64 * hf + 64, :, :], in_=w_v[(2 * job[2] + hf) * 4 + job[1]])
                else:
                    nc.sync.dma_start(out=t[:], in_=x_v[job[1]])
                raws[job] = t

        def s1(n, i, a0=0, a1=2):
            if not ok(n):
                return
            gt = S1_ORDER[i]
            if (n, gt) not in av:
                pool = afp if gt == GF else avp
                av[(n, gt)] = pool.tile([P, 2, WC, 2], F32, name="a%d" % gt, tag="a%d" % gt)
            nc.scalar.activation(
                out=av[(n, gt)][:, a0:a1, :, :],
                in_=zr[(n, gt)][:, 2 * a0:2 * a1, :].rearrange("p (a e) c -> p a c e", e=2),
                func=(AF.Tanh if gt == GG else AF.Sigmoid),
            )

        def chain_a(n, which=(0, 1, 2, 3, 4, 5), a0=0, a1=2):
            if not ok(n):
                return
            hc = n % 4
            if n not in tt:
                tn = {}
                for i in range(1, 6):
                    tn[i] = tp.tile([P, 2, WC, 2], F32, name="t%d" % i, tag="t%d" % i)
                tt[n] = tn
            t = {}
            for i in range(1, 6):
                t[i] = tt[n][i][:, a0:a1, :, :]
            z = {}
            for gt in (GI, GF, GG, GO):
                z[gt] = av[(n, gt)][:, a0:a1, :, :]
            for i in which:
                if i == 0:
                    mul(t[1], z[GI], z[GG])
                elif i == 1:
                    mul(t[2], z[GF], c0b[:, hc * WC:(hc + 1) * WC].unsqueeze(1).unsqueeze(3).to_broadcast([P, a1 - a0, WC, 2]))
                elif i == 2:
                    mul(t[5], z[GO], zr[(n, GOUT)][:, 2 * a0:2 * a1, :].rearrange("p (a e) c -> p a c e", e=2))
                elif i == 3:
                    nc.vector.tensor_tensor(out=t[3], in0=t[1], in1=t[2], op=ALU.add)
                elif i == 4:
                    stt(t[1], z[GI], -1.0, t[1])
                else:
                    stt(t[2], z[GF], -1.0, t[2])

        def s3(n, part):
            if not ok(n):
                return
            t = tt[n]
            gg = av[(n, GG)]
            if part == 0:
                nc.scalar.activation(out=gg[:], in_=gg[:], func=AF.Square)
            elif part == 1:
                nc.scalar.activation(out=t[3][:], in_=t[3][:], func=AF.Tanh, scale=-1.0)
            else:
                nc.scalar.activation(out=t[4][:], in_=t[3][:], func=AF.Square)

        def last(dz, lo, in0, in1):
            mul(
                dz[:, lo:lo + WC, :].rearrange("p c (a e) -> p c a e", e=2),
                in0[:].rearrange("p a c e -> p c a e"),
                in1[:].rearrange("p a c e -> p c a e"),
            )

        def chain_b(n, which=(0, 1, 2, 3, 4, 5, 6)):
            if not ok(n):
                return
            t = tt[n]
            ai, gg, ao = av[(n, GI)], av[(n, GG)], av[(n, GO)]
            if which[0] == 0:
                dz0 = dzp.tile([P, 2 * WC, J], BF16, name="dz0", tag="dz0", align_bytes=64)
                dz1 = dzp.tile([P, 2 * WC, J], BF16, name="dz1", tag="dz1", align_bytes=64)
                dzt[n] = (dz0, dz1)
            dz0, dz1 = dzt[n]
            for i in which:
                if i == 0:
                    stt(ao[:], ao[:], -1.0, t[3][:])
                elif i == 1:
                    stt(t[4][:], t[4][:], -1.0, t[5][:])
                elif i == 2:
                    last(dz1, WC, ao, t[5])
                elif i == 3:
                    stt(gg[:], gg[:], -1.0, ai[:])
                elif i == 4:
                    last(dz0, 0, t[1], t[4])
                elif i == 5:
                    last(dz1, 0, gg, t[4])
                else:
                    last(dz0, WC, t[2], t[4])

        def tr(n, s):
            if not ok(n):
                return
            words = dzt[n][s][:].rearrange("p c j -> p (c j)").bitcast(F32)
            bl = []
            for a in (0, 1):
                bank = ps_tp.tile([P, 4 * P], F32, name="tpb", tag="tpb")
                for t in range(4):
                    nc.tensor.transpose(bank[:, t * P:(t + 1) * P], words[:, 2 * t + a:4 * WC:8], ident[:])
                bl.append(bank)
            banks[(n, s)] = bl

        def ef(n, s, engs=(0, 0)):
            if not ok(n):
                return
            bl = banks.pop((n, s))
            ql = []
            for a in (0, 1):
                qf = qfp.tile([P, 8 * P], BF16, name="qf", tag="qf", align_bytes=64)
                copy_on(
                    engs[a],
                    qf[:].rearrange("p (e r t) -> p e r t", e=2, t=4),
                    bl[a][:].bitcast(BF16).rearrange("p (t r e) -> p e r t", t=4, e=2),
                )
                ql.append(qf)
            qfs[(n, s)] = ql

        def qf_(n, s):
            if not ok(n):
                return
            ql = qfs.pop((n, s))
            fl = []
            for a in (0, 1):
                fc = fcp.tile([P, 2 * P], U32, name="fc", tag="fc", align_bytes=64)
                fs = fcp.tile([P, 2 * P], U8, name="fs", tag="fs", align_bytes=64)
                nc.vector.quantize_mx(out=fc[:].bitcast(E5), scales=fs[:], in_=ql[a][:])
                fl.append((fc, fs))
            fcs[(n, s)] = fl

        def mf(n, s):
            if not ok(n):
                return
            hc = n % 4
            if hc == 0 and s == 1:
                for j in range(J):
                    acc[j] = ps_acc.tile([P, IN], F32, name="acc%d" % j, tag="acc%d" % j)
            fl = fcs.pop((n, s))
            wc, ws = opnd[("w", hc, s)]
            for a in (0, 1):
                fc, fs = fl[a]
                for e in (0, 1):
                    nc.tensor.matmul_mx(
                        out=acc[2 * a + e][:],
                        lhsT=fc[:, e * P:(e + 1) * P].bitcast(E5),
                        lhsT_scale=fs[:, e * P:(e + 1) * P],
                        rhs=wc[:].bitcast(E4),
                        rhs_scale=ws[:],
                        start=(hc == 0 and s == 1),
                        stop=(hc == 3 and s == 0),
                    )

        def store(dst, src_psum, eng):
            o = outp.tile([P, IN], F32, name="os", tag="os")
            copy_on(eng, o[:], src_psum[:])
            nc.sync.dma_start(out=dst, in_=o[:])

        def e0(g, j, eng):
            store(out0_v[g, j], acc[j], eng)

        def qt(n, s):
            if not ok(n):
                return
            g, hc = n // 4, n % 4
            if g == 0:
                nm = "%d%d" % (hc, s)
                cod = keep.tile([P, IN], U32, name="k0c" + nm, tag="k0c" + nm, align_bytes=64)
                sca = keep.tile([P, IN], U8, name="k0s" + nm, tag="k0s" + nm, align_bytes=64)
                k0[(hc, s)] = (cod, sca)
            else:
                cod = k1p.tile([P, IN], U32, name="k1c", tag="k1c", align_bytes=64)
                sca = k1p.tile([P, IN], U8, name="k1s", tag="k1s", align_bytes=64)
                k1[(hc, s)] = (cod, sca)
            nc.vector.quantize_mx(out=cod[:].bitcast(E5), scales=sca[:], in_=dzt[n][s][:].rearrange("p c j -> p (c j)"))

        def mt(n, i, parts=(0, 1), spare=False):
            if not ok(n) or n < 4:
                return
            hc = n % 4
            s, m = 1 - i // 4, i % 4
            if parts[0] == 0:
                if spare:
                    o1s[(n, i)] = ps_tp.tile([P, IN], F32, name="tpb", tag="tpb")
                else:
                    o1s[(n, i)] = ps_o1.tile([P, IN], F32, name="o1", tag="o1")
            o1 = o1s[(n, i)]
            for gg in parts:
                kc, ks = (k0 if gg == 0 else k1)[(hc, s)]
                xc, xs = opnd[("x", gg, 0)]
                nc.tensor.matmul_mx(
                    out=o1[:],
                    lhsT=kc[:, m * P:(m + 1) * P].bitcast(E5),
                    lhsT_scale=ks[:, m * P:(m + 1) * P],
                    rhs=xc[:].bitcast(E4),
                    rhs_scale=xs[:],
                    start=(gg == 0),
                    stop=(gg == 1),
                )

        def eo(n, i, eng=0):
            if not ok(n) or n < 4:
                return
            hc = n % 4
            s, m = 1 - i // 4, i % 4
            store(out1_v[(2 * s + m // 2) * 8 + hc * 2 + m % 2], o1s.pop((n, i)), eng)

        def jobs_a(k):
            dv = DV_JOB.get(k, 0)
            for job in JOBS.get(k, ()):
                il = ilp.tile([P, IN, J], BF16, name="il", tag="il", align_bytes=64)
                ils[job] = il
                nc.scalar.copy(
                    out=il[:, dv:IN, :].rearrange("p (c i) j -> p c j i", i=4),
                    in_=raws[job][:, :, dv:IN].rearrange("p j (c i) -> p c j i", i=4),
                )

        def jobs_d(k):
            dv = DV_JOB.get(k, 0)
            for job in JOBS.get(k, ()):
                if dv > 0:
                    nc.vector.tensor_copy(
                        out=ils[job][:, 0:dv, :].rearrange("p (c i) j -> p c j i", i=4),
                        in_=raws[job][:, :, 0:dv].rearrange("p j (c i) -> p c j i", i=4),
                    )

        def jobs_q(k):
            for job in JOBS.get(k, ()):
                nm = "%s%d%d" % job
                cod = keep.tile([P, IN], U32, name="c" + nm, tag="c" + nm, align_bytes=64)
                sca = keep.tile([P, IN], U8, name="s" + nm, tag="s" + nm, align_bytes=64)
                nc.vector.quantize_mx(out=cod[:].bitcast(E4), scales=sca[:], in_=ils.pop(job)[:].rearrange("p c j -> p (c j)"))
                opnd[job] = (cod, sca)

        c0row = keep.tile([P, HID], BF16, name="c0row", tag="c0row")
        nc.vector.memset(c0row[:], 0.0)
        ld(0, GI, 0, 1)
        ld(0, GG, 0, 1)
        nc.sync.dma_start(out=c0row[0:1, :], in_=c_init.rearrange("(o n) -> o n", o=1))
        for gt in (GF, GO, GOUT):
            ld(0, gt, 0, 1)
        for gt in (GI, GG, GF, GO, GOUT):
            ld(0, gt, 1, 2)
        warm = keep.tile([P, 1], F32, name="warm", tag="warm")
        nc.gpsimd.memset(warm[:], 0.0)
        nc.scalar.activation(out=warm[:], in_=warm[:], func=AF.Sigmoid)
        ones = keep.tile([P, P], BF16, name="ones", tag="ones")
        nc.vector.memset(ones[:], 1.0)
        ident = keep.tile([P, P], F32, name="ident", tag="ident")
        masks.make_identity(nc, ident[:])
        c0b = keep.tile([P, HID], BF16, name="c0b", tag="c0b")
        c0ps = []
        for h in (0, 1):
            bank = ps_tp.tile([P, 4 * P], F32, name="tpb", tag="tpb")
            nc.tensor.matmul(bank[:], lhsT=ones[:], rhs=c0row[:, h * 512:(h + 1) * 512], start=True, stop=True)
            c0ps.append(bank)

        def c0_piece(lo, hi, eng):
            copy_on(eng, c0b[:, lo:hi], c0ps[lo // 512][:, lo % 512:lo % 512 + hi - lo])

        for i in range(4):
            lent = tp.tile([P, 2, WC, 2], F32, name="t%d" % (i + 1), tag="t%d" % (i + 1))
            zr[(1, S1_ORDER[i])] = lent[:].rearrange("p a c e -> p (a c e)").rearrange("p (j c) -> p j c", j=J)
            ld(1, S1_ORDER[i])
        ld(1, GOUT)
        for a in (0, 1):
            for i in range(4):
                s1(0, i, a, a + 1)
                if a == 1:
                    ld(2, S1_ORDER[i])
        chain_a(0, (0,), 0, 1)
        c0_piece(0, WC, 1)
        chain_a(0, (1, 2, 3, 4, 5), 0, 1)
        chain_a(0, a0=1, a1=2)
        ld(2, GOUT)
        c0_piece(WC, 512, 0)
        c0_piece(512, 1024, 0)
        for i in range(4):
            s1(1, i)
        ld_jobs(0)
        for i in range(3):
            s3(0, i)

        for k in range(0, NSTEP - 1):
            ef(k - 1, 1)
            tr(k - 1, 0)
            qt(k - 1, 1)
            qt(k - 1, 0)
            mt(k - 1, 0)
            mt(k - 1, 1)
            chain_a(k + 1, (0, 1, 2, 3))
            ld(k + 3, GOUT)
            chain_b(k, (0,))
            chain_a(k + 1, (4, 5))
            if 1 <= k <= 4:
                jobs_q(k - 1)
            s1(k + 2, 0)
            ld(k + 3, S1_ORDER[0])
            eo(k - 1, 0)
            mt(k - 1, 2)
            s1(k + 2, 1)
            ld(k + 3, S1_ORDER[1])
            eo(k - 1, 1)
            mt(k - 1, 3)
            ef(k - 1, 0)
            chain_b(k, (1, 2, 3, 4, 5, 6))
            eo(k - 1, 2)
            mt(k - 1, 4)
            s1(k + 2, 2)
            ld(k + 3, S1_ORDER[2])
            eo(k - 1, 3)
            mt(k - 1, 5)
            s1(k + 2, 3)
            ld(k + 3, S1_ORDER[3])
            if k == 5:
                for j in range(J):
                    e0(0, j, 0)
            eo(k - 1, 4)
            mt(k - 1, 6)
            s3(k + 1, 0)
            eo(k - 1, 5)
            mt(k - 1, 7)
            s3(k + 1, 1)
            eo(k - 1, 6)
            jobs_a(k)
            s3(k + 1, 2)
            eo(k - 1, 7)
            tr(k, 1)
            jobs_d(k)
            qf_(k - 1, 1)
            qf_(k - 1, 0)
            mf(k - 1, 1)
            mf(k - 1, 0)
            if k == 4:
                jobs_q(k)
            ld_jobs(k + 1)

        ef(6, 1)
        qt(6, 1)
        qt(6, 0)
        mt(6, 0)
        mt(6, 1)
        tr(6, 0)
        chain_b(7, (0, 1))
        eo(6, 0)
        mt(6, 2)
        eo(6, 1)
        mt(6, 3)
        qf_(6, 1)
        mf(6, 1)
        chain_b(7, (2, 3))
        ef(6, 0)
        eo(6, 2)
        mt(6, 4)
        eo(6, 3)
        mt(6, 5)
        chain_b(7, (5,))
        tr(7, 1)
        qf_(6, 0)
        mf(6, 0)
        chain_b(7, (4,))
        eo(6, 4)
        mt(6, 6)
        eo(6, 5)
        mt(6, 7)
        qt(7, 1)
        chain_b(7, (6,))
        ef(7, 1, (0, 1))
        tr(7, 0)
        eo(6, 6, 0)
        mt(7, 0)
        eo(6, 7, 0)
        mt(7, 1)
        qf_(7, 1)
        mf(7, 1)
        qt(7, 0)
        ef(7, 0, (0, 1))
        mt(7, 2, (0, 1), True)
        mt(7, 3, (0, 1), True)
        qf_(7, 0)
        mf(7, 0)
        eo(7, 0, 0)
        mt(7, 4)
        eo(7, 1, 1)
        mt(7, 5)
        eo(7, 2, 0)
        mt(7, 6, (0, 1), True)
        eo(7, 3, 1)
        mt(7, 7, (0, 1), True)
        e0(1, 0, 0)
        e0(1, 1, 1)
        e0(1, 2, 0)
        e0(1, 3, 1)
        eo(7, 4, 0)
        eo(7, 5, 1)
        eo(7, 6, 0)
        eo(7, 7, 1)
